import numpy as np
import ml_dtypes


def mxq(x, axis, fmt="e4m3"):
    dtype, down = {"e4m3": (ml_dtypes.float8_e4m3fn, 7), "e5m2": (ml_dtypes.float8_e5m2, 14)}[fmt]
    v = np.moveaxis(np.asarray(x, np.float32).astype(ml_dtypes.bfloat16).astype(np.float64), axis, -1)
    blocks = v.reshape(v.shape[:-1] + (-1, 32))
    amax = np.abs(blocks).max(-1, keepdims=True)
    byte = np.maximum(np.where(amax > 0, np.frexp(amax)[1] - 1 + 127, 0) - down, 1)
    scale = np.exp2(byte - 127.0)
    codes = (blocks / scale).astype(np.float32).astype(dtype).astype(np.float64)
    return np.moveaxis((codes * scale).reshape(v.shape), -1, axis)


WIDE = False


def mx_kscale(k):
    if not WIDE:
        return np.ones(k)
    levels = np.array([10, -10, 5, -5, 0])
    if k % 512:
        return np.exp2(np.random.permutation(np.resize(levels, k // 32))).repeat(32)
    a = np.empty((k // 512, 16))
    for p in range(k // 512):
        a[p, :8] = np.random.permutation(np.resize(levels, 8))
        for g in range(8):
            far = levels[np.abs(levels - a[p, g]) >= 10]
            a[p, g + 8] = far[np.random.randint(len(far))]
    return np.exp2(a.ravel()).repeat(32)


BF16 = ml_dtypes.bfloat16


def bf(x):
    return np.asarray(x, np.float32).astype(BF16)


def f64(x):
    return np.asarray(x).astype(np.float64)


B, L, D, NC, DS = 2, 128, 1024, 2, 4
EPS = 2.0 ** -23


def rmsnorm(v, w):
    ms = np.mean(np.square(v), axis=-1, keepdims=True)
    return v * (1.0 / np.sqrt(ms + EPS)) * w


def setup_inputs():
    s = mx_kscale(D)
    s = s / s.max()
    t = mx_kscale(NC * D)
    tc = t.reshape(NC, D, 1)
    return {"x": bf(np.random.standard_normal((B, L, D)) * s),
            "W_in": bf(np.random.standard_normal((NC * D, D)) / np.sqrt(D) / s[None, :]),
            "W_out": bf(np.random.standard_normal((D, NC * D)) / np.sqrt(NC * D) / t[None, :]),
            "A_theta": bf(np.random.standard_normal((NC, D, DS)) * 0.5),
            "B_real": bf(np.random.standard_normal((NC, D, DS))),
            "B_imag": bf(np.random.standard_normal((NC, D, DS))),
            "C_real": bf(np.random.standard_normal((NC, D, DS)) / np.sqrt(2 * DS) * tc),
            "C_imag": bf(np.random.standard_normal((NC, D, DS)) / np.sqrt(2 * DS) * tc),
            "norm_w": bf(1.0 + 0.1 * np.random.standard_normal(D))}


def reference(x, W_in, W_out, A_theta, B_real, B_imag, C_real, C_imag, norm_w):
    x = f64(x)
    b, l, _ = x.shape
    xi = (mxq(x, 2, "e4m3") @ mxq(f64(W_in), 1, "e4m3").T).reshape(b, l, NC, D)[..., None]
    ct = np.cos(f64(A_theta))
    st = np.sin(f64(A_theta))
    rs = np.zeros((b, l, NC, D, DS))
    is_ = np.zeros_like(rs)
    bxr = f64(B_real) * xi
    bxi = f64(B_imag) * xi
    nr = ct * rs - st * is_ + bxr
    ni = st * rs + ct * is_ + bxi
    y = np.sum(f64(C_real) * nr - f64(C_imag) * ni, axis=-1)
    out = mxq(y.reshape(b, l, NC * D), 2, "e4m3") @ mxq(f64(W_out), 1, "e4m3").T
    return x + rmsnorm(out, f64(norm_w)), nr, ni

@@ -1,0 +1,467 @@
+from contextlib import ExitStack
+
+import concourse.mybir as mybir
+from concourse.masks import make_identity
+
+F32 = mybir.dt.float32
+BF16 = mybir.dt.bfloat16
+U32 = mybir.dt.uint32
+U8 = mybir.dt.uint8
+FP8X4 = mybir.dt.float8_e4m3fn_x4
+ALU = mybir.AluOpType
+ACT = mybir.ActivationFunctionType
+
+P = 128
+TOKENS = 256
+TOKEN_TILES = TOKENS // P
+D_MODEL = 1024
+FEATURES = 2048
+STATES = 4
+EPS = 2.0**-23
+
+K_PASS = 512
+PASS_WORDS = K_PASS // 2
+BANK = 512
+
+ROUNDS = 4
+CHUNK = FEATURES // ROUNDS
+IN_PASSES = D_MODEL // K_PASS
+OUT_PASSES = FEATURES // K_PASS
+OUT_COLS = D_MODEL // ROUNDS
+CHUNK_WORDS = 1024
+
+WEIGHT_CHUNKS = 2 * ROUNDS
+Y_OPERAND = WEIGHT_CHUNKS
+AHEAD = 3
+SHARED_FROM = 2
+
+TABLE_ROW = 2 * P
+TABLE_ROWS = FEATURES * STATES // TABLE_ROW
+NORM_W_ROW = 2 * TABLE_ROWS
+
+FLOPS = 2 * TOKENS * D_MODEL * FEATURES * 2
+
+
+def tile_mamba3core_kernel(
+    tc, x, W_in, W_out, A_theta, B_real, B_imag, C_real, C_imag, norm_w, out_0, out_1, out_2
+):
+    nc = tc.nc
+    x_rows = x.flatten_outer_dims()
+    res_rows = out_0.flatten_outer_dims()
+    state_rows = [
+        out_1.rearrange("b l c d n -> (b l) (c d n)"),
+        out_2.rearrange("b l c d n -> (b l) (c d n)"),
+    ]
+    b_flat = [B_real.rearrange("c d n -> (c d n)"), B_imag.rearrange("c d n -> (c d n)")]
+    c_flat = [C_real.rearrange("c d n -> (c d n)"), C_imag.rearrange("c d n -> (c d n)")]
+
+    with ExitStack() as ctx:
+        keep = ctx.enter_context(tc.tile_pool(name="keep", bufs=1))
+        weights = ctx.enter_context(tc.tile_pool(name="weights", bufs=4))
+        grouping = ctx.enter_context(tc.tile_pool(name="grouping", bufs=3))
+        staging = ctx.enter_context(tc.tile_pool(name="staging", bufs=7))
+        y_rows = ctx.enter_context(tc.tile_pool(name="y_rows", bufs=2))
+        xi_copies = ctx.enter_context(tc.tile_pool(name="xi_copies", bufs=2))
+        small = ctx.enter_context(tc.tile_pool(name="small", bufs=2))
+        xi_banks = ctx.enter_context(tc.psum_pool(name="xi_banks", bufs=4))
+        work_banks = ctx.enter_context(tc.psum_pool(name="work_banks", bufs=4))
+        ctx.enter_context(tc.manual_schedule())
+
+        ident = keep.tile([P, P], F32)
+        table = keep.tile([P, TABLE_ROW], BF16)
+        table_columns = keep.tile([P, P], F32)
+        b_real_all = keep.tile([P, FEATURES * STATES // 2], F32)
+        b_imag_all = keep.tile([P, FEATURES * STATES // 2], F32)
+        b_all = [b_real_all, b_imag_all]
+        b_feats = keep.tile([P, 2, ROUNDS, 4 * STATES], BF16)
+        c_feats = keep.tile([P, 2, ROUNDS, 4 * STATES], BF16)
+        gain_terms = keep.tile([P, 2, ROUNDS * 4 * STATES], F32)
+        gain_diff = keep.tile([P, ROUNDS * 4, STATES], F32)
+        gain_half = keep.tile([P, ROUNDS * 4, 2], F32)
+        gain = keep.tile([P, FEATURES // P], F32)
+        minus_half = keep.tile([P, 1], F32)
+        norm_w_all = keep.tile([P, D_MODEL // 2], F32)
+        x_sb = keep.tile([P, TOKEN_TILES * D_MODEL], BF16)
+        x_grouped = keep.tile([P, IN_PASSES * TOKENS, 2], F32, align_bytes=64)
+        y_grouped = keep.tile([P, OUT_PASSES * TOKENS * 4], BF16, align_bytes=64)
+        x_codes = keep.tile([P, IN_PASSES * TOKENS], U32, align_bytes=64)
+        x_scales = keep.tile([P, IN_PASSES * TOKENS], U8, align_bytes=64)
+        y_codes = keep.tile([P, OUT_PASSES * TOKENS], U32, align_bytes=64)
+        y_scales = keep.tile([P, OUT_PASSES * TOKENS], U8, align_bytes=64)
+        win_codes = keep.tile([P, ROUNDS, CHUNK_WORDS], U32, align_bytes=64)
+        win_scales = keep.tile([P, ROUNDS, CHUNK_WORDS], U8, align_bytes=64)
+        wout_codes = keep.tile([P, ROUNDS, CHUNK_WORDS], U32, align_bytes=64)
+        wout_scales = keep.tile([P, ROUNDS, CHUNK_WORDS], U8, align_bytes=64)
+
+        loaded = {}
+        grouped_of = {}
+        xi_of = {}
+        shared_of = {}
+        acc_of = {}
+        rstd_of = {}
+        tiles_of_round = [(t, part) for t in range(TOKEN_TILES) for part in range(2)]
+
+        def load_weights(n):
+            w_sb = weights.tile([P, 4 * CHUNK_WORDS], BF16, tag="w_sb")
+            if n < ROUNDS:
+                nc.sync.dma_start(
+                    out=w_sb[:].rearrange("p (j k) -> p j k", j=4),
+                    in_=W_in[n * CHUNK : (n + 1) * CHUNK, :].rearrange("(p j) k -> p j k", j=4),
+                )
+            else:
+                first = (n - ROUNDS) * OUT_COLS
+                nc.sync.dma_start(
+                    out=w_sb[:].rearrange("p (i f) -> p i f", i=2),
+                    in_=W_out[first : first + OUT_COLS, :].rearrange("(i p) f -> p i f", p=P),
+                )
+            loaded[n] = w_sb
+
+        def k_to_partitions(rows_sb, row_tiles, passes, grouped, copies):
+            words = rows_sb.bitcast(F32)
+            row_words = passes * PASS_WORDS
+            pairs = row_tiles // 2
+            for k_pass in range(passes):
+                for pair in range(pairs):
+                    bank = work_banks.tile([P, BANK], F32, tag="bank")
+                    for h in range(2):
+                        for s in range(2):
+                            first = (2 * pair + s) * row_words + k_pass * PASS_WORDS
+                            nc.tensor.transpose(
+                                out=bank[:, (2 * h + s) * P : (2 * h + s + 1) * P],
+                                in_=words[:, first + h : first + PASS_WORDS : 2],
+                                identity=ident[:],
+                            )
+                    b = k_pass * pairs + pair
+                    column = b * 2 * P
+                    copies[b % len(copies)](
+                        out=grouped[:, column : column + 2 * P, :],
+                        in_=bank[:].rearrange("p (h c) -> p c h", h=2),
+                    )
+
+        def prepare_weights(n, copies):
+            grouped = grouping.tile([P, CHUNK_WORDS, 2], F32, tag="grouped", align_bytes=64)
+            passes = IN_PASSES if n < ROUNDS else OUT_PASSES
+            k_to_partitions(loaded[n][:], 8 // passes, passes, grouped, copies)
+            grouped_of[n] = grouped[:].rearrange("p c h -> p (c h)").bitcast(BF16)
+            if n + ROUNDS < WEIGHT_CHUNKS:
+                load_weights(n + ROUNDS)
+
+        def quantise(n):
+            if n < ROUNDS:
+                codes, scales = win_codes[:, n, :], win_scales[:, n, :]
+            elif n < WEIGHT_CHUNKS:
+                codes, scales = wout_codes[:, n - ROUNDS, :], wout_scales[:, n - ROUNDS, :]
+            else:
+                codes, scales = y_codes[:], y_scales[:]
+            nc.vector.quantize_mx(out=codes.bitcast(FP8X4), scales=scales, in_=grouped_of[n])
+
+        def mx_pass(acc, a_codes, a_scales, b_codes, b_scales, first, last):
+            nc.tensor.matmul_mx(
+                out=acc,
+                lhsT=a_codes.bitcast(FP8X4),
+                lhsT_scale=a_scales,
+                rhs=b_codes.bitcast(FP8X4),
+                rhs_scale=b_scales,
+                start=first,
+                stop=last,
+            )
+
+        def spread_table_rows(first_row, dest, copy):
+            bank = work_banks.tile([P, BANK], F32, tag="bank")
+            for i in range(4):
+                row = first_row + i
+                nc.tensor.transpose(
+                    out=bank[:, i * P : (i + 1) * P],
+                    in_=table_columns[:, row : row + 1].to_broadcast([P, P]),
+                    identity=ident[:],
+                )
+            copy(out=dest, in_=bank[:])
+
+        def spread_b(r, copy):
+            for part in range(2):
+                for h in range(2):
+                    block = 2 * r + h
+                    spread_table_rows(
+                        part * TABLE_ROWS + 4 * block,
+                        b_all[part][:, block * BANK : (block + 1) * BANK],
+                        copy,
+                    )
+
+        def xi_by_token(r):
+            for t in range(TOKEN_TILES):
+                xi = xi_banks.tile([P, CHUNK], F32, tag="xi")
+                for k_pass in range(IN_PASSES):
+                    toks = slice(k_pass * TOKENS + t * P, k_pass * TOKENS + (t + 1) * P)
+                    feats = slice(k_pass * CHUNK, (k_pass + 1) * CHUNK)
+                    mx_pass(
+                        xi[:],
+                        x_codes[:, toks],
+                        x_scales[:, toks],
+                        win_codes[:, r, feats],
+                        win_scales[:, r, feats],
+                        k_pass == 0,
+                        k_pass == IN_PASSES - 1,
+                    )
+                xi_of[(r, t)] = xi
+
+        def b_values(r, h, part):
+            width = 2 * P * STATES
+            first = (2 * r + h) * width
+            return b_all[part][:].bitcast(BF16)[:, first : first + width]
+
+        def gpsimd_share(r):
+            xi_sb = xi_copies.tile([P, TOKEN_TILES, 2 * P], F32, tag="xi_sb")
+            for t in range(TOKEN_TILES):
+                nc.scalar.copy(
+                    out=xi_sb[:, t, :].rearrange("t (q j) -> t q j", j=4),
+                    in_=xi_of[(r, t)][:].rearrange("t (j q) -> t q j", j=4)[:, P // 2 : P, :],
+                )
+            for t, part in tiles_of_round[1:]:
+                prod = staging.tile([P, CHUNK * STATES], F32, tag="stage")
+                nc.gpsimd.tensor_tensor(
+                    out=prod[:, CHUNK * STATES // 2 :].rearrange("t (f n) -> t f n", n=STATES),
+                    in0=xi_sb[:, t, :].unsqueeze(2).to_broadcast([P, 2 * P, STATES]),
+                    in1=b_values(r, 1, part).rearrange("t (f n) -> t f n", n=STATES),
+                    op=ALU.mult,
+                )
+                shared_of[(r, t, part)] = prod
+
+        def state_products(r, t, part):
+            if (r, t, part) in shared_of:
+                prod = shared_of[(r, t, part)]
+                halves = [0]
+            else:
+                prod = staging.tile([P, CHUNK * STATES], F32, tag="stage")
+                halves = [0, 1]
+            width = 2 * P * STATES
+            for h in halves:
+                xi_quads = xi_of[(r, t)][:].rearrange("t (j q) -> t q j", j=4)[
+                    :, h * P // 2 : (h + 1) * P // 2, :
+                ]
+                nc.vector.tensor_tensor(
+                    out=prod[:, h * width : (h + 1) * width].rearrange(
+                        "t (q j n) -> t q j n", j=4, n=STATES
+                    ),
+                    in0=xi_quads.unsqueeze(3).to_broadcast([P, P // 2, 4, STATES]),
+                    in1=b_values(r, h, part).rearrange("t (q j n) -> t q j n", j=4, n=STATES),
+                    op=ALU.mult,
+                )
+            nc.sync.dma_start(
+                out=state_rows[part][
+                    t * P : (t + 1) * P, r * CHUNK * STATES : (r + 1) * CHUNK * STATES
+                ],
+                in_=prod[:],
+            )
+
+        def gain_on_partitions():
+            for part in range(2):
+                nc.gpsimd.tensor_tensor(
+                    out=gain_terms[:, part, :],
+                    in0=c_feats[:, part, :, :].rearrange("p r w -> p (r w)"),
+                    in1=b_feats[:, part, :, :].rearrange("p r w -> p (r w)"),
+                    op=ALU.mult,
+                )
+            nc.gpsimd.tensor_tensor(
+                out=gain_diff[:].rearrange("p f n -> p (f n)"),
+                in0=gain_terms[:, 0, :],
+                in1=gain_terms[:, 1, :],
+                op=ALU.subtract,
+            )
+            nc.gpsimd.tensor_tensor(
+                out=gain_half[:], in0=gain_diff[:, :, 0:2], in1=gain_diff[:, :, 2:4], op=ALU.add
+            )
+            nc.gpsimd.tensor_tensor(
+                out=gain[:], in0=gain_half[:, :, 0], in1=gain_half[:, :, 1], op=ALU.add
+            )
+
+        def y_of_round(r):
+            y_lin = y_rows.tile([P, 4, TOKENS], BF16, tag="y_lin")
+            for pair in range(2):
+                bank = work_banks.tile([P, BANK], F32, tag="bank")
+                for s in range(2):
+                    j = 2 * pair + s
+                    for k_pass in range(IN_PASSES):
+                        feats = slice(k_pass * CHUNK + j * P, k_pass * CHUNK + (j + 1) * P)
+                        toks = slice(k_pass * TOKENS, (k_pass + 1) * TOKENS)
+                        mx_pass(
+                            bank[:, s * TOKENS : (s + 1) * TOKENS],
+                            win_codes[:, r, feats],
+                            win_scales[:, r, feats],
+                            x_codes[:, toks],
+                            x_scales[:, toks],
+                            k_pass == 0,
+                            k_pass == IN_PASSES - 1,
+                        )
+                for s in range(2):
+                    j = 2 * pair + s
+                    nc.scalar.activation(
+                        out=y_lin[:, j, :],
+                        in_=bank[:, s * TOKENS : (s + 1) * TOKENS],
+                        func=ACT.Copy,
+                        scale=gain[:, 4 * r + j : 4 * r + j + 1],
+                    )
+            nc.gpsimd.tensor_scalar(
+                out=y_grouped[:, r * 4 * TOKENS : (r + 1) * 4 * TOKENS].rearrange(
+                    "p (t j) -> p t j", j=4
+                ),
+                in0=y_lin[:].rearrange("p j t -> p t j"),
+                scalar1=1.0,
+                scalar2=0.0,
+                op0=ALU.mult,
+                op1=ALU.add,
+            )
+
+        def second_matmul():
+            for t in range(TOKEN_TILES):
+                for half in range(2):
+                    acc = work_banks.tile([P, BANK], F32, tag="bank")
+                    for s in range(2):
+                        chunk = 2 * half + s
+                        for k_pass in range(OUT_PASSES):
+                            toks = slice(k_pass * TOKENS + t * P, k_pass * TOKENS + (t + 1) * P)
+                            cols = slice(k_pass * OUT_COLS, (k_pass + 1) * OUT_COLS)
+                            mx_pass(
+                                acc[:, s * OUT_COLS : (s + 1) * OUT_COLS],
+                                y_codes[:, toks],
+                                y_scales[:, toks],
+                                wout_codes[:, chunk, cols],
+                                wout_scales[:, chunk, cols],
+                                k_pass == 0,
+                                k_pass == OUT_PASSES - 1,
+                            )
+                    acc_of[(t, half)] = acc
+
+        def one_over_rms():
+            for t in range(TOKEN_TILES):
+                sumsq = small.tile([P, 2], F32, tag="sumsq")
+                total = small.tile([P, 1], F32, tag="total")
+                mean_eps = small.tile([P, 1], F32, tag="mean_eps")
+                rstd = small.tile([P, 1], F32, tag="rstd")
+                for half in range(2):
+                    unused = (2 * t + half) * BANK
+                    nc.scalar.activation(
+                        out=y_grouped[:, unused : unused + BANK],
+                        in_=acc_of[(t, half)][:],
+                        func=ACT.Square,
+                        accum_out=sumsq[:, half : half + 1],
+                    )
+                nc.gpsimd.tensor_tensor(
+                    out=total[:], in0=sumsq[:, 0:1], in1=sumsq[:, 1:2], op=ALU.add
+                )
+                nc.gpsimd.tensor_scalar(
+                    out=mean_eps[:],
+                    in0=total[:],
+                    scalar1=1.0 / D_MODEL,
+                    scalar2=EPS,
+                    op0=ALU.mult,
+                    op1=ALU.add,
+                )
+                nc.gpsimd.tensor_tensor(
+                    out=rstd[:], in0=mean_eps[:], in1=minus_half[:], op=ALU.pow
+                )
+                rstd_of[t] = rstd
+
+        def finish_rows(t):
+            final = staging.tile([P, 2 * D_MODEL], F32, tag="stage")
+            norm_w_values = norm_w_all[:].bitcast(BF16)
+            for half in range(2):
+                cols = slice(half * BANK, (half + 1) * BANK)
+                nc.vector.scalar_tensor_tensor(
+                    out=final[:, cols],
+                    in0=acc_of[(t, half)][:],
+                    scalar=rstd_of[t][:, 0:1],
+                    in1=norm_w_values[:, cols],
+                    op0=ALU.mult,
+                    op1=ALU.mult,
+                )
+            nc.vector.tensor_tensor(
+                out=final[:, D_MODEL : 2 * D_MODEL],
+                in0=final[:, 0:D_MODEL],
+                in1=x_sb[:, t * D_MODEL : (t + 1) * D_MODEL],
+                op=ALU.add,
+            )
+            nc.scalar.dma_start(
+                out=res_rows[t * P : (t + 1) * P, :], in_=final[:, D_MODEL : 2 * D_MODEL]
+            )
+
+        def after_quantise(n):
+            if n + AHEAD < WEIGHT_CHUNKS:
+                prepare_weights(n + AHEAD, [nc.scalar.copy])
+            if n < ROUNDS:
+                y_of_round(n)
+
+        make_identity(nc, ident[:])
+        nc.gpsimd.memset(minus_half[:], -0.5)
+        nc.vector.memset(table[NORM_W_ROW:P, :], 0.0)
+
+        for part in range(2):
+            nc.sync.dma_start(
+                out=table[part * TABLE_ROWS : (part + 1) * TABLE_ROWS, :],
+                in_=b_flat[part].rearrange("(r w) -> r w", w=TABLE_ROW),
+            )
+        nc.sync.dma_start(
+            out=table[NORM_W_ROW : NORM_W_ROW + 4, :],
+            in_=norm_w.rearrange("(r w) -> r w", w=TABLE_ROW),
+        )
+        nc.sync.dma_start(
+            out=x_sb[:].rearrange("p (t k) -> p t k", t=TOKEN_TILES),
+            in_=x_rows.rearrange("(t p) k -> p t k", p=P),
+        )
+        for n in range(ROUNDS):
+            load_weights(n)
+        for part in range(2):
+            nc.scalar.dma_start(
+                out=b_feats[:, part, :, :],
+                in_=b_flat[part].rearrange("(r p w) -> p r w", p=P, w=4 * STATES),
+            )
+            nc.scalar.dma_start(
+                out=c_feats[:, part, :, :],
+                in_=c_flat[part].rearrange("(r p w) -> p r w", p=P, w=4 * STATES),
+            )
+
+        gain_on_partitions()
+
+        both = [nc.scalar.copy, nc.vector.tensor_copy]
+        bank = work_banks.tile([P, BANK], F32, tag="bank")
+        nc.tensor.transpose(out=bank[:, 0:P], in_=table[:].bitcast(F32), identity=ident[:])
+        nc.vector.tensor_copy(out=table_columns[:], in_=bank[:, 0:P])
+        spread_b(0, nc.vector.tensor_copy)
+        k_to_partitions(x_sb[:], TOKEN_TILES, IN_PASSES, x_grouped, both)
+        nc.vector.quantize_mx(
+            out=x_codes[:].bitcast(FP8X4),
+            scales=x_scales[:],
+            in_=x_grouped[:].rearrange("p c h -> p (c h)").bitcast(BF16),
+        )
+        prepare_weights(0, both)
+        for n in range(1, AHEAD):
+            prepare_weights(n, [nc.scalar.copy])
+        quantise(0)
+        xi_by_token(0)
+        prepare_weights(AHEAD, [nc.scalar.copy])
+        y_of_round(0)
+        grouped_of[Y_OPERAND] = y_grouped[:]
+
+        for r in range(ROUNDS):
+            for i in range(len(tiles_of_round)):
+                t, part = tiles_of_round[i]
+                state_products(r, t, part)
+                n = r * len(tiles_of_round) + i + 1
+                if n < WEIGHT_CHUNKS:
+                    quantise(n)
+                    after_quantise(n)
+                if n == WEIGHT_CHUNKS - 1:
+                    quantise(Y_OPERAND)
+                    spread_table_rows(NORM_W_ROW, norm_w_all[:], nc.scalar.copy)
+                    second_matmul()
+                    one_over_rms()
+                if i == 0 and r + 1 < ROUNDS:
+                    xi_by_token(r + 1)
+                    if r == 0:
+                        spread_b(1, nc.scalar.copy)
+                    if r == 1:
+                        spread_b(2, nc.scalar.copy)
+                        spread_b(3, nc.scalar.copy)
+                    if r + 1 >= SHARED_FROM:
+                        gpsimd_share(r + 1)
+        for t in range(TOKEN_TILES):
+            finish_rows(t)

@@ -33,11 +33,11 @@ CHUNK_WORDS = 1024
 WEIGHT_CHUNKS = 2 * ROUNDS
 Y_OPERAND = WEIGHT_CHUNKS
 AHEAD = 3
-SHARED_FROM = 2
+VECTOR_TILES = 3
 
 TABLE_ROW = 2 * P
 TABLE_ROWS = FEATURES * STATES // TABLE_ROW
-NORM_W_ROW = 2 * TABLE_ROWS
+NORM_W_ROWS = D_MODEL // TABLE_ROW
 
 FLOPS = 2 * TOKENS * D_MODEL * FEATURES * 2
 
@@ -57,9 +57,8 @@ def tile_mamba3core_kernel(
 
     with ExitStack() as ctx:
         keep = ctx.enter_context(tc.tile_pool(name="keep", bufs=1))
-        weights = ctx.enter_context(tc.tile_pool(name="weights", bufs=4))
         grouping = ctx.enter_context(tc.tile_pool(name="grouping", bufs=3))
-        staging = ctx.enter_context(tc.tile_pool(name="staging", bufs=7))
+        staging = ctx.enter_context(tc.tile_pool(name="staging", bufs=12))
         y_rows = ctx.enter_context(tc.tile_pool(name="y_rows", bufs=2))
         xi_copies = ctx.enter_context(tc.tile_pool(name="xi_copies", bufs=2))
         small = ctx.enter_context(tc.tile_pool(name="small", bufs=2))
@@ -70,6 +69,8 @@ def tile_mamba3core_kernel(
         ident = keep.tile([P, P], F32)
         table = keep.tile([P, TABLE_ROW], BF16)
         table_columns = keep.tile([P, P], F32)
+        norm_w_rows = keep.tile([P, TABLE_ROW], BF16)
+        norm_w_columns = keep.tile([P, 4], F32)
         b_real_all = keep.tile([P, FEATURES * STATES // 2], F32)
         b_imag_all = keep.tile([P, FEATURES * STATES // 2], F32)
         b_all = [b_real_all, b_imag_all]
@@ -79,11 +80,13 @@ def tile_mamba3core_kernel(
         gain_diff = keep.tile([P, ROUNDS * 4, STATES], F32)
         gain_half = keep.tile([P, ROUNDS * 4, 2], F32)
         gain = keep.tile([P, FEATURES // P], F32)
-        minus_half = keep.tile([P, 1], F32)
+        minus_half = keep.tile([P, TOKEN_TILES], F32)
+        rstd = keep.tile([P, TOKEN_TILES], F32)
         norm_w_all = keep.tile([P, D_MODEL // 2], F32)
         x_sb = keep.tile([P, TOKEN_TILES * D_MODEL], BF16)
         x_grouped = keep.tile([P, IN_PASSES * TOKENS, 2], F32, align_bytes=64)
         y_grouped = keep.tile([P, OUT_PASSES * TOKENS * 4], BF16, align_bytes=64)
+        gates = keep.tile([P, WEIGHT_CHUNKS], U32)
         x_codes = keep.tile([P, IN_PASSES * TOKENS], U32, align_bytes=64)
         x_scales = keep.tile([P, IN_PASSES * TOKENS], U8, align_bytes=64)
         y_codes = keep.tile([P, OUT_PASSES * TOKENS], U32, align_bytes=64)
@@ -96,55 +99,55 @@ def tile_mamba3core_kernel(
         loaded = {}
         grouped_of = {}
         xi_of = {}
-        shared_of = {}
+        gpsimd_xi = {}
+        gpsimd_tile = {}
+        y_lin_of = {}
         acc_of = {}
-        rstd_of = {}
         tiles_of_round = [(t, part) for t in range(TOKEN_TILES) for part in range(2)]
 
-        def load_weights(n):
-            w_sb = weights.tile([P, 4 * CHUNK_WORDS], BF16, tag="w_sb")
+        def load_weights(n, parts=1):
+            w_sb = staging.tile([P, 4 * CHUNK_WORDS], BF16, tag="stage")
             if n < ROUNDS:
-                nc.sync.dma_start(
-                    out=w_sb[:].rearrange("p (j k) -> p j k", j=4),
-                    in_=W_in[n * CHUNK : (n + 1) * CHUNK, :].rearrange("(p j) k -> p j k", j=4),
-                )
+                by_row = w_sb[:].rearrange("p (j k) -> p j k", j=4)
+                rows = W_in[n * CHUNK : (n + 1) * CHUNK, :].rearrange("(p j) k -> p j k", j=4)
             else:
                 first = (n - ROUNDS) * OUT_COLS
-                nc.sync.dma_start(
-                    out=w_sb[:].rearrange("p (i f) -> p i f", i=2),
-                    in_=W_out[first : first + OUT_COLS, :].rearrange("(i p) f -> p i f", p=P),
-                )
+                by_row = w_sb[:].rearrange("p (i f) -> p i f", i=2)
+                rows = W_out[first : first + OUT_COLS, :].rearrange("(i p) f -> p i f", p=P)
+            width = rows.shape[2] // parts
+            for part in range(parts):
+                cols = slice(part * width, (part + 1) * width)
+                nc.sync.dma_start(out=by_row[:, :, cols], in_=rows[:, :, cols])
             loaded[n] = w_sb
 
-        def k_to_partitions(rows_sb, row_tiles, passes, grouped, copies):
+        def k_to_partitions(rows_sb, row_tiles, passes, k_pass, grouped, copies):
             words = rows_sb.bitcast(F32)
             row_words = passes * PASS_WORDS
             pairs = row_tiles // 2
-            for k_pass in range(passes):
-                for pair in range(pairs):
-                    bank = work_banks.tile([P, BANK], F32, tag="bank")
-                    for h in range(2):
-                        for s in range(2):
-                            first = (2 * pair + s) * row_words + k_pass * PASS_WORDS
-                            nc.tensor.transpose(
-                                out=bank[:, (2 * h + s) * P : (2 * h + s + 1) * P],
-                                in_=words[:, first + h : first + PASS_WORDS : 2],
-                                identity=ident[:],
-                            )
-                    b = k_pass * pairs + pair
-                    column = b * 2 * P
-                    copies[b % len(copies)](
-                        out=grouped[:, column : column + 2 * P, :],
-                        in_=bank[:].rearrange("p (h c) -> p c h", h=2),
-                    )
+            for pair in range(pairs):
+                bank = work_banks.tile([P, BANK], F32, tag="bank")
+                for h in range(2):
+                    for s in range(2):
+                        first = (2 * pair + s) * row_words + k_pass * PASS_WORDS
+                        nc.tensor.transpose(
+                            out=bank[:, (2 * h + s) * P : (2 * h + s + 1) * P],
+                            in_=words[:, first + h : first + PASS_WORDS : 2],
+                            identity=ident[:],
+                        )
+                b = k_pass * pairs + pair
+                column = b * 2 * P
+                copies[b % len(copies)](
+                    out=grouped[:, column : column + 2 * P, :],
+                    in_=bank[:].rearrange("p (h c) -> p c h", h=2),
+                )
 
-        def prepare_weights(n, copies):
+        def prepare_weights(n, copies_of_pass):
             grouped = grouping.tile([P, CHUNK_WORDS, 2], F32, tag="grouped", align_bytes=64)
             passes = IN_PASSES if n < ROUNDS else OUT_PASSES
-            k_to_partitions(loaded[n][:], 8 // passes, passes, grouped, copies)
+            for k_pass in range(passes):
+                copies = copies_of_pass[k_pass % len(copies_of_pass)]
+                k_to_partitions(loaded[n][:], 8 // passes, passes, k_pass, grouped, copies)
             grouped_of[n] = grouped[:].rearrange("p c h -> p (c h)").bitcast(BF16)
-            if n + ROUNDS < WEIGHT_CHUNKS:
-                load_weights(n + ROUNDS)
 
         def quantise(n):
             if n < ROUNDS:
@@ -166,13 +169,13 @@ def tile_mamba3core_kernel(
                 stop=last,
             )
 
-        def spread_table_rows(first_row, dest, copy):
+        def spread_rows(columns, first_row, dest, copy):
             bank = work_banks.tile([P, BANK], F32, tag="bank")
             for i in range(4):
                 row = first_row + i
                 nc.tensor.transpose(
                     out=bank[:, i * P : (i + 1) * P],
-                    in_=table_columns[:, row : row + 1].to_broadcast([P, P]),
+                    in_=columns[:, row : row + 1].to_broadcast([P, P]),
                     identity=ident[:],
                 )
             copy(out=dest, in_=bank[:])
@@ -181,7 +184,8 @@ def tile_mamba3core_kernel(
             for part in range(2):
                 for h in range(2):
                     block = 2 * r + h
-                    spread_table_rows(
+                    spread_rows(
+                        table_columns,
                         part * TABLE_ROWS + 4 * block,
                         b_all[part][:, block * BANK : (block + 1) * BANK],
                         copy,
@@ -209,32 +213,46 @@ def tile_mamba3core_kernel(
             first = (2 * r + h) * width
             return b_all[part][:].bitcast(BF16)[:, first : first + width]
 
-        def gpsimd_share(r):
-            xi_sb = xi_copies.tile([P, TOKEN_TILES, 2 * P], F32, tag="xi_sb")
-            for t in range(TOKEN_TILES):
-                nc.scalar.copy(
-                    out=xi_sb[:, t, :].rearrange("t (q j) -> t q j", j=4),
-                    in_=xi_of[(r, t)][:].rearrange("t (j q) -> t q j", j=4)[:, P // 2 : P, :],
-                )
-            for t, part in tiles_of_round[1:]:
-                prod = staging.tile([P, CHUNK * STATES], F32, tag="stage")
-                nc.gpsimd.tensor_tensor(
-                    out=prod[:, CHUNK * STATES // 2 :].rearrange("t (f n) -> t f n", n=STATES),
-                    in0=xi_sb[:, t, :].unsqueeze(2).to_broadcast([P, 2 * P, STATES]),
-                    in1=b_values(r, 1, part).rearrange("t (f n) -> t f n", n=STATES),
-                    op=ALU.mult,
-                )
-                shared_of[(r, t, part)] = prod
+        def xi_for_gpsimd(r):
+            xi_sb = xi_copies.tile([P, CHUNK], F32, tag="xi_sb")
+            t = TOKEN_TILES - 1
+            nc.scalar.copy(
+                out=xi_sb[:].rearrange("t (q j) -> t q j", j=4),
+                in_=xi_of[(r, t)][:].rearrange("t (j q) -> t q j", j=4),
+            )
+            gpsimd_xi[r] = xi_sb
+            prod = staging.tile([P, CHUNK * STATES], F32, tag="stage")
+            gpsimd_tile[r] = prod
+
+        def gate(n):
+            codes = win_codes[:, n, 0:1] if n < ROUNDS else wout_codes[:, n - ROUNDS, 0:1]
+            nc.gpsimd.tensor_copy(out=gates[:, n : n + 1], in_=codes)
+
+        def gpsimd_product(r, h):
+            width = 2 * P * STATES
+            nc.gpsimd.tensor_tensor(
+                out=gpsimd_tile[r][:, h * width : (h + 1) * width].rearrange(
+                    "t (f n) -> t f n", n=STATES
+                ),
+                in0=gpsimd_xi[r][:, h * 2 * P : (h + 1) * 2 * P]
+                .unsqueeze(2)
+                .to_broadcast([P, 2 * P, STATES]),
+                in1=b_values(r, h, 1).rearrange("t (f n) -> t f n", n=STATES),
+                op=ALU.mult,
+            )
+
+        def store_products(r, t, part, prod):
+            nc.sync.dma_start(
+                out=state_rows[part][
+                    t * P : (t + 1) * P, r * CHUNK * STATES : (r + 1) * CHUNK * STATES
+                ],
+                in_=prod[:],
+            )
 
         def state_products(r, t, part):
-            if (r, t, part) in shared_of:
-                prod = shared_of[(r, t, part)]
-                halves = [0]
-            else:
-                prod = staging.tile([P, CHUNK * STATES], F32, tag="stage")
-                halves = [0, 1]
+            prod = staging.tile([P, CHUNK * STATES], F32, tag="stage")
             width = 2 * P * STATES
-            for h in halves:
+            for h in range(2):
                 xi_quads = xi_of[(r, t)][:].rearrange("t (j q) -> t q j", j=4)[
                     :, h * P // 2 : (h + 1) * P // 2, :
                 ]
@@ -246,12 +264,7 @@ def tile_mamba3core_kernel(
                     in1=b_values(r, h, part).rearrange("t (q j n) -> t q j n", j=4, n=STATES),
                     op=ALU.mult,
                 )
-            nc.sync.dma_start(
-                out=state_rows[part][
-                    t * P : (t + 1) * P, r * CHUNK * STATES : (r + 1) * CHUNK * STATES
-                ],
-                in_=prod[:],
-            )
+            store_products(r, t, part, prod)
 
         def gain_on_partitions():
             for part in range(2):
@@ -300,11 +313,14 @@ def tile_mamba3core_kernel(
                         func=ACT.Copy,
                         scale=gain[:, 4 * r + j : 4 * r + j + 1],
                     )
+            y_lin_of[r] = y_lin
+
+        def interleave_y(r):
             nc.gpsimd.tensor_scalar(
                 out=y_grouped[:, r * 4 * TOKENS : (r + 1) * 4 * TOKENS].rearrange(
                     "p (t j) -> p t j", j=4
                 ),
-                in0=y_lin[:].rearrange("p j t -> p t j"),
+                in0=y_lin_of[r][:].rearrange("p j t -> p t j"),
                 scalar1=1.0,
                 scalar2=0.0,
                 op0=ALU.mult,
@@ -331,35 +347,35 @@ def tile_mamba3core_kernel(
                             )
                     acc_of[(t, half)] = acc
 
-        def one_over_rms():
+        def sums_of_squares():
+            sumsq = keep.tile([P, TOKEN_TILES * 2], F32)
             for t in range(TOKEN_TILES):
-                sumsq = small.tile([P, 2], F32, tag="sumsq")
-                total = small.tile([P, 1], F32, tag="total")
-                mean_eps = small.tile([P, 1], F32, tag="mean_eps")
-                rstd = small.tile([P, 1], F32, tag="rstd")
                 for half in range(2):
-                    unused = (2 * t + half) * BANK
+                    b = 2 * t + half
                     nc.scalar.activation(
-                        out=y_grouped[:, unused : unused + BANK],
+                        out=y_grouped[:, b * BANK : (b + 1) * BANK],
                         in_=acc_of[(t, half)][:],
                         func=ACT.Square,
-                        accum_out=sumsq[:, half : half + 1],
+                        accum_out=sumsq[:, b : b + 1],
                     )
-                nc.gpsimd.tensor_tensor(
-                    out=total[:], in0=sumsq[:, 0:1], in1=sumsq[:, 1:2], op=ALU.add
-                )
-                nc.gpsimd.tensor_scalar(
-                    out=mean_eps[:],
-                    in0=total[:],
-                    scalar1=1.0 / D_MODEL,
-                    scalar2=EPS,
-                    op0=ALU.mult,
-                    op1=ALU.add,
-                )
-                nc.gpsimd.tensor_tensor(
-                    out=rstd[:], in0=mean_eps[:], in1=minus_half[:], op=ALU.pow
-                )
-                rstd_of[t] = rstd
+            return sumsq
+
+        def one_over_rms(sumsq):
+            total = small.tile([P, TOKEN_TILES], F32, tag="total")
+            mean_eps = small.tile([P, TOKEN_TILES], F32, tag="mean_eps")
+            by_half = sumsq[:].rearrange("p (t h) -> p t h", h=2)
+            nc.gpsimd.tensor_tensor(
+                out=total[:], in0=by_half[:, :, 0], in1=by_half[:, :, 1], op=ALU.add
+            )
+            nc.gpsimd.tensor_scalar(
+                out=mean_eps[:],
+                in0=total[:],
+                scalar1=1.0 / D_MODEL,
+                scalar2=EPS,
+                op0=ALU.mult,
+                op1=ALU.add,
+            )
+            nc.gpsimd.tensor_tensor(out=rstd[:], in0=mean_eps[:], in1=minus_half[:], op=ALU.pow)
 
         def finish_rows(t):
             final = staging.tile([P, 2 * D_MODEL], F32, tag="stage")
@@ -369,7 +385,7 @@ def tile_mamba3core_kernel(
                 nc.vector.scalar_tensor_tensor(
                     out=final[:, cols],
                     in0=acc_of[(t, half)][:],
-                    scalar=rstd_of[t][:, 0:1],
+                    scalar=rstd[:, t : t + 1],
                     in1=norm_w_values[:, cols],
                     op0=ALU.mult,
                     op1=ALU.mult,
@@ -384,40 +400,47 @@ def tile_mamba3core_kernel(
                 out=res_rows[t * P : (t + 1) * P, :], in_=final[:, D_MODEL : 2 * D_MODEL]
             )
 
-        def after_quantise(n):
-            if n + AHEAD < WEIGHT_CHUNKS:
-                prepare_weights(n + AHEAD, [nc.scalar.copy])
-            if n < ROUNDS:
-                y_of_round(n)
+        def spread_norm_w():
+            bank = work_banks.tile([P, BANK], F32, tag="bank")
+            nc.tensor.transpose(
+                out=bank[:, 0:P], in_=norm_w_rows[:].bitcast(F32), identity=ident[:]
+            )
+            nc.scalar.copy(out=norm_w_columns[:], in_=bank[:, 0:NORM_W_ROWS])
+            spread_rows(norm_w_columns, 0, norm_w_all[:], nc.scalar.copy)
+
+        def store_gpsimd_tile(r):
+            store_products(r, TOKEN_TILES - 1, 1, gpsimd_tile[r])
 
         make_identity(nc, ident[:])
         nc.gpsimd.memset(minus_half[:], -0.5)
-        nc.vector.memset(table[NORM_W_ROW:P, :], 0.0)
+        nc.vector.memset(table[2 * TABLE_ROWS : P, :], 0.0)
+        nc.vector.memset(norm_w_rows[:], 0.0)
 
         for part in range(2):
-            nc.sync.dma_start(
+            nc.scalar.dma_start(
                 out=table[part * TABLE_ROWS : (part + 1) * TABLE_ROWS, :],
                 in_=b_flat[part].rearrange("(r w) -> r w", w=TABLE_ROW),
             )
         nc.sync.dma_start(
-            out=table[NORM_W_ROW : NORM_W_ROW + 4, :],
-            in_=norm_w.rearrange("(r w) -> r w", w=TABLE_ROW),
-        )
-        nc.sync.dma_start(
             out=x_sb[:].rearrange("p (t k) -> p t k", t=TOKEN_TILES),
             in_=x_rows.rearrange("(t p) k -> p t k", p=P),
         )
-        for n in range(ROUNDS):
-            load_weights(n)
+        load_weights(0, parts=IN_PASSES)
+        load_weights(1)
         for part in range(2):
-            nc.scalar.dma_start(
+            nc.sync.dma_start(
                 out=b_feats[:, part, :, :],
                 in_=b_flat[part].rearrange("(r p w) -> p r w", p=P, w=4 * STATES),
             )
-            nc.scalar.dma_start(
+            nc.sync.dma_start(
                 out=c_feats[:, part, :, :],
                 in_=c_flat[part].rearrange("(r p w) -> p r w", p=P, w=4 * STATES),
             )
+        for n in range(2, WEIGHT_CHUNKS):
+            load_weights(n)
+        nc.sync.dma_start(
+            out=norm_w_rows[0:NORM_W_ROWS, :], in_=norm_w.rearrange("(r w) -> r w", w=TABLE_ROW)
+        )
 
         gain_on_partitions()
 
@@ -425,43 +448,81 @@ def tile_mamba3core_kernel(
         bank = work_banks.tile([P, BANK], F32, tag="bank")
         nc.tensor.transpose(out=bank[:, 0:P], in_=table[:].bitcast(F32), identity=ident[:])
         nc.vector.tensor_copy(out=table_columns[:], in_=bank[:, 0:P])
-        spread_b(0, nc.vector.tensor_copy)
-        k_to_partitions(x_sb[:], TOKEN_TILES, IN_PASSES, x_grouped, both)
+        for k_pass in range(IN_PASSES):
+            k_to_partitions(x_sb[:], TOKEN_TILES, IN_PASSES, k_pass, x_grouped, both)
+        prepare_weights(0, [both, [nc.scalar.copy]])
         nc.vector.quantize_mx(
             out=x_codes[:].bitcast(FP8X4),
             scales=x_scales[:],
             in_=x_grouped[:].rearrange("p c h -> p (c h)").bitcast(BF16),
         )
-        prepare_weights(0, both)
-        for n in range(1, AHEAD):
-            prepare_weights(n, [nc.scalar.copy])
-        quantise(0)
+        for k_pass in range(IN_PASSES):
+            cols = slice(k_pass * CHUNK, (k_pass + 1) * CHUNK)
+            nc.vector.quantize_mx(
+                out=win_codes[:, 0, cols].bitcast(FP8X4),
+                scales=win_scales[:, 0, cols],
+                in_=grouped_of[0][:, k_pass * 4 * CHUNK : (k_pass + 1) * 4 * CHUNK],
+            )
+        spread_b(0, nc.scalar.copy)
         xi_by_token(0)
-        prepare_weights(AHEAD, [nc.scalar.copy])
-        y_of_round(0)
+        xi_for_gpsimd(0)
+        for n in range(1, AHEAD + 1):
+            prepare_weights(n, [[nc.scalar.copy]])
         grouped_of[Y_OPERAND] = y_grouped[:]
 
-        for r in range(ROUNDS):
-            for i in range(len(tiles_of_round)):
-                t, part = tiles_of_round[i]
-                state_products(r, t, part)
-                n = r * len(tiles_of_round) + i + 1
-                if n < WEIGHT_CHUNKS:
-                    quantise(n)
-                    after_quantise(n)
-                if n == WEIGHT_CHUNKS - 1:
-                    quantise(Y_OPERAND)
-                    spread_table_rows(NORM_W_ROW, norm_w_all[:], nc.scalar.copy)
-                    second_matmul()
-                    one_over_rms()
-                if i == 0 and r + 1 < ROUNDS:
-                    xi_by_token(r + 1)
-                    if r == 0:
-                        spread_b(1, nc.scalar.copy)
-                    if r == 1:
-                        spread_b(2, nc.scalar.copy)
-                        spread_b(3, nc.scalar.copy)
-                    if r + 1 >= SHARED_FROM:
-                        gpsimd_share(r + 1)
+        for step in range(ROUNDS * VECTOR_TILES):
+            r, i = divmod(step, VECTOR_TILES)
+            t, part = tiles_of_round[i]
+            state_products(r, t, part)
+            n = step + 1
+            if n <= WEIGHT_CHUNKS:
+                quantise(n)
+            if n < WEIGHT_CHUNKS:
+                gate(n)
+            if n + AHEAD < WEIGHT_CHUNKS:
+                prepare_weights(n + AHEAD, [[nc.scalar.copy]])
+            if step == 0:
+                gpsimd_product(0, 0)
+                xi_by_token(1)
+                spread_b(1, nc.scalar.copy)
+            elif step == 1:
+                gpsimd_product(0, 1)
+                y_of_round(0)
+            elif step == 2:
+                store_gpsimd_tile(0)
+                xi_for_gpsimd(1)
+                interleave_y(0)
+            elif step == 3:
+                gpsimd_product(1, 0)
+                y_of_round(1)
+                xi_by_token(2)
+            elif step == 4:
+                gpsimd_product(1, 1)
+                spread_b(2, nc.scalar.copy)
+                y_of_round(2)
+            elif step == 5:
+                store_gpsimd_tile(1)
+                interleave_y(1)
+                xi_for_gpsimd(2)
+                y_of_round(3)
+                interleave_y(2)
+            elif step == 6:
+                interleave_y(3)
+                xi_by_token(3)
+                spread_b(3, nc.scalar.copy)
+                spread_norm_w()
+                xi_for_gpsimd(3)
+            elif step == 7:
+                gpsimd_product(2, 0)
+                gpsimd_product(2, 1)
+                second_matmul()
+            elif step == 8:
+                sumsq = sums_of_squares()
+                gpsimd_product(3, 0)
+                one_over_rms(sumsq)
+                gpsimd_product(3, 1)
+            elif step == 9:
+                store_gpsimd_tile(2)
+        store_gpsimd_tile(3)
         for t in range(TOKEN_TILES):
             finish_rows(t)

@@ -33,7 +33,6 @@ CHUNK_WORDS = 1024
 WEIGHT_CHUNKS = 2 * ROUNDS
 Y_OPERAND = WEIGHT_CHUNKS
 AHEAD = 3
-VECTOR_TILES = 3
 
 TABLE_ROW = 2 * P
 TABLE_ROWS = FEATURES * STATES // TABLE_ROW
@@ -60,10 +59,9 @@ def tile_mamba3core_kernel(
         grouping = ctx.enter_context(tc.tile_pool(name="grouping", bufs=3))
         staging = ctx.enter_context(tc.tile_pool(name="staging", bufs=12))
         y_rows = ctx.enter_context(tc.tile_pool(name="y_rows", bufs=2))
-        xi_copies = ctx.enter_context(tc.tile_pool(name="xi_copies", bufs=2))
         small = ctx.enter_context(tc.tile_pool(name="small", bufs=2))
-        xi_banks = ctx.enter_context(tc.psum_pool(name="xi_banks", bufs=4))
-        work_banks = ctx.enter_context(tc.psum_pool(name="work_banks", bufs=4))
+        xi_banks = ctx.enter_context(tc.psum_pool(name="xi_banks", bufs=3))
+        work_banks = ctx.enter_context(tc.psum_pool(name="work_banks", bufs=5))
         ctx.enter_context(tc.manual_schedule())
 
         ident = keep.tile([P, P], F32)
@@ -86,7 +84,6 @@ def tile_mamba3core_kernel(
         x_sb = keep.tile([P, TOKEN_TILES * D_MODEL], BF16)
         x_grouped = keep.tile([P, IN_PASSES * TOKENS, 2], F32, align_bytes=64)
         y_grouped = keep.tile([P, OUT_PASSES * TOKENS * 4], BF16, align_bytes=64)
-        gates = keep.tile([P, WEIGHT_CHUNKS], U32)
         x_codes = keep.tile([P, IN_PASSES * TOKENS], U32, align_bytes=64)
         x_scales = keep.tile([P, IN_PASSES * TOKENS], U8, align_bytes=64)
         y_codes = keep.tile([P, OUT_PASSES * TOKENS], U32, align_bytes=64)
@@ -99,8 +96,6 @@ def tile_mamba3core_kernel(
         loaded = {}
         grouped_of = {}
         xi_of = {}
-        gpsimd_xi = {}
-        gpsimd_tile = {}
         y_lin_of = {}
         acc_of = {}
         tiles_of_round = [(t, part) for t in range(TOKEN_TILES) for part in range(2)]
@@ -141,13 +136,13 @@ def tile_mamba3core_kernel(
                     in_=bank[:].rearrange("p (h c) -> p c h", h=2),
                 )
 
-        def prepare_weights(n, copies_of_pass):
-            grouped = grouping.tile([P, CHUNK_WORDS, 2], F32, tag="grouped", align_bytes=64)
+        def prepare_weights(n, copies, k_passes):
+            if n not in grouped_of:
+                grouped = grouping.tile([P, CHUNK_WORDS, 2], F32, tag="grouped", align_bytes=64)
+                grouped_of[n] = grouped
             passes = IN_PASSES if n < ROUNDS else OUT_PASSES
-            for k_pass in range(passes):
-                copies = copies_of_pass[k_pass % len(copies_of_pass)]
-                k_to_partitions(loaded[n][:], 8 // passes, passes, k_pass, grouped, copies)
-            grouped_of[n] = grouped[:].rearrange("p c h -> p (c h)").bitcast(BF16)
+            for k_pass in k_passes:
+                k_to_partitions(loaded[n][:], 8 // passes, passes, k_pass, grouped_of[n], copies)
 
         def quantise(n):
             if n < ROUNDS:
@@ -156,7 +151,19 @@ def tile_mamba3core_kernel(
                 codes, scales = wout_codes[:, n - ROUNDS, :], wout_scales[:, n - ROUNDS, :]
             else:
                 codes, scales = y_codes[:], y_scales[:]
-            nc.vector.quantize_mx(out=codes.bitcast(FP8X4), scales=scales, in_=grouped_of[n])
+            if n == Y_OPERAND:
+                values = y_grouped[:]
+            else:
+                values = grouped_of[n][:].rearrange("p c h -> p (c h)").bitcast(BF16)
+            nc.vector.quantize_mx(out=codes.bitcast(FP8X4), scales=scales, in_=values)
+
+        def quantise_pass_of_chunk_0(k_pass):
+            cols = slice(k_pass * CHUNK, (k_pass + 1) * CHUNK)
+            nc.vector.quantize_mx(
+                out=win_codes[:, 0, cols].bitcast(FP8X4),
+                scales=win_scales[:, 0, cols],
+                in_=grouped_of[0][:, cols, :].rearrange("p c h -> p (c h)").bitcast(BF16),
+            )
 
         def mx_pass(acc, a_codes, a_scales, b_codes, b_scales, first, last):
             nc.tensor.matmul_mx(
@@ -191,55 +198,26 @@ def tile_mamba3core_kernel(
                         copy,
                     )
 
-        def xi_by_token(r):
-            for t in range(TOKEN_TILES):
-                xi = xi_banks.tile([P, CHUNK], F32, tag="xi")
-                for k_pass in range(IN_PASSES):
-                    toks = slice(k_pass * TOKENS + t * P, k_pass * TOKENS + (t + 1) * P)
-                    feats = slice(k_pass * CHUNK, (k_pass + 1) * CHUNK)
-                    mx_pass(
-                        xi[:],
-                        x_codes[:, toks],
-                        x_scales[:, toks],
-                        win_codes[:, r, feats],
-                        win_scales[:, r, feats],
-                        k_pass == 0,
-                        k_pass == IN_PASSES - 1,
-                    )
-                xi_of[(r, t)] = xi
+        def xi_by_token(r, t):
+            xi = xi_banks.tile([P, CHUNK], F32, tag="xi")
+            for k_pass in range(IN_PASSES):
+                toks = slice(k_pass * TOKENS + t * P, k_pass * TOKENS + (t + 1) * P)
+                feats = slice(k_pass * CHUNK, (k_pass + 1) * CHUNK)
+                mx_pass(
+                    xi[:],
+                    x_codes[:, toks],
+                    x_scales[:, toks],
+                    win_codes[:, r, feats],
+                    win_scales[:, r, feats],
+                    k_pass == 0,
+                    k_pass == IN_PASSES - 1,
+                )
+            xi_of[(r, t)] = xi
 
         def b_values(r, h, part):
             width = 2 * P * STATES
             first = (2 * r + h) * width
             return b_all[part][:].bitcast(BF16)[:, first : first + width]
-
-        def xi_for_gpsimd(r):
-            xi_sb = xi_copies.tile([P, CHUNK], F32, tag="xi_sb")
-            t = TOKEN_TILES - 1
-            nc.scalar.copy(
-                out=xi_sb[:].rearrange("t (q j) -> t q j", j=4),
-                in_=xi_of[(r, t)][:].rearrange("t (j q) -> t q j", j=4),
-            )
-            gpsimd_xi[r] = xi_sb
-            prod = staging.tile([P, CHUNK * STATES], F32, tag="stage")
-            gpsimd_tile[r] = prod
-
-        def gate(n):
-            codes = win_codes[:, n, 0:1] if n < ROUNDS else wout_codes[:, n - ROUNDS, 0:1]
-            nc.gpsimd.tensor_copy(out=gates[:, n : n + 1], in_=codes)
-
-        def gpsimd_product(r, h):
-            width = 2 * P * STATES
-            nc.gpsimd.tensor_tensor(
-                out=gpsimd_tile[r][:, h * width : (h + 1) * width].rearrange(
-                    "t (f n) -> t f n", n=STATES
-                ),
-                in0=gpsimd_xi[r][:, h * 2 * P : (h + 1) * 2 * P]
-                .unsqueeze(2)
-                .to_broadcast([P, 2 * P, STATES]),
-                in1=b_values(r, h, 1).rearrange("t (f n) -> t f n", n=STATES),
-                op=ALU.mult,
-            )
 
         def store_products(r, t, part, prod):
             nc.sync.dma_start(
@@ -408,9 +386,6 @@ def tile_mamba3core_kernel(
             nc.scalar.copy(out=norm_w_columns[:], in_=bank[:, 0:NORM_W_ROWS])
             spread_rows(norm_w_columns, 0, norm_w_all[:], nc.scalar.copy)
 
-        def store_gpsimd_tile(r):
-            store_products(r, TOKEN_TILES - 1, 1, gpsimd_tile[r])
-
         make_identity(nc, ident[:])
         nc.gpsimd.memset(minus_half[:], -0.5)
         nc.vector.memset(table[2 * TABLE_ROWS : P, :], 0.0)
@@ -445,84 +420,91 @@ def tile_mamba3core_kernel(
         gain_on_partitions()
 
         both = [nc.scalar.copy, nc.vector.tensor_copy]
-        bank = work_banks.tile([P, BANK], F32, tag="bank")
-        nc.tensor.transpose(out=bank[:, 0:P], in_=table[:].bitcast(F32), identity=ident[:])
-        nc.vector.tensor_copy(out=table_columns[:], in_=bank[:, 0:P])
         for k_pass in range(IN_PASSES):
             k_to_partitions(x_sb[:], TOKEN_TILES, IN_PASSES, k_pass, x_grouped, both)
-        prepare_weights(0, [both, [nc.scalar.copy]])
+        prepare_weights(0, both, [0])
         nc.vector.quantize_mx(
             out=x_codes[:].bitcast(FP8X4),
             scales=x_scales[:],
             in_=x_grouped[:].rearrange("p c h -> p (c h)").bitcast(BF16),
         )
-        for k_pass in range(IN_PASSES):
-            cols = slice(k_pass * CHUNK, (k_pass + 1) * CHUNK)
-            nc.vector.quantize_mx(
-                out=win_codes[:, 0, cols].bitcast(FP8X4),
-                scales=win_scales[:, 0, cols],
-                in_=grouped_of[0][:, k_pass * 4 * CHUNK : (k_pass + 1) * 4 * CHUNK],
-            )
+        quantise_pass_of_chunk_0(0)
+        bank = work_banks.tile([P, BANK], F32, tag="bank")
+        nc.tensor.transpose(out=bank[:, 0:P], in_=table[:].bitcast(F32), identity=ident[:])
+        nc.scalar.copy(out=table_columns[:], in_=bank[:, 0:P])
+        prepare_weights(0, both, [1])
+        quantise_pass_of_chunk_0(1)
         spread_b(0, nc.scalar.copy)
-        xi_by_token(0)
-        xi_for_gpsimd(0)
-        for n in range(1, AHEAD + 1):
-            prepare_weights(n, [[nc.scalar.copy]])
-        grouped_of[Y_OPERAND] = y_grouped[:]
+        xi_by_token(0, 0)
+        xi_by_token(0, 1)
 
-        for step in range(ROUNDS * VECTOR_TILES):
-            r, i = divmod(step, VECTOR_TILES)
+        def W(n, v=()):
+            copies = [nc.vector.tensor_copy if b in v else nc.scalar.copy for b in range(4)]
+            prepare_weights(n, copies, range(IN_PASSES if n < ROUNDS else OUT_PASSES))
+
+        def VP(r, i):
             t, part = tiles_of_round[i]
             state_products(r, t, part)
-            n = step + 1
-            if n <= WEIGHT_CHUNKS:
-                quantise(n)
-            if n < WEIGHT_CHUNKS:
-                gate(n)
-            if n + AHEAD < WEIGHT_CHUNKS:
-                prepare_weights(n + AHEAD, [[nc.scalar.copy]])
-            if step == 0:
-                gpsimd_product(0, 0)
-                xi_by_token(1)
-                spread_b(1, nc.scalar.copy)
-            elif step == 1:
-                gpsimd_product(0, 1)
-                y_of_round(0)
-            elif step == 2:
-                store_gpsimd_tile(0)
-                xi_for_gpsimd(1)
-                interleave_y(0)
-            elif step == 3:
-                gpsimd_product(1, 0)
-                y_of_round(1)
-                xi_by_token(2)
-            elif step == 4:
-                gpsimd_product(1, 1)
-                spread_b(2, nc.scalar.copy)
-                y_of_round(2)
-            elif step == 5:
-                store_gpsimd_tile(1)
-                interleave_y(1)
-                xi_for_gpsimd(2)
-                y_of_round(3)
-                interleave_y(2)
-            elif step == 6:
-                interleave_y(3)
-                xi_by_token(3)
-                spread_b(3, nc.scalar.copy)
-                spread_norm_w()
-                xi_for_gpsimd(3)
-            elif step == 7:
-                gpsimd_product(2, 0)
-                gpsimd_product(2, 1)
-                second_matmul()
-            elif step == 8:
-                sumsq = sums_of_squares()
-                gpsimd_product(3, 0)
-                one_over_rms(sumsq)
-                gpsimd_product(3, 1)
-            elif step == 9:
-                store_gpsimd_tile(2)
-        store_gpsimd_tile(3)
-        for t in range(TOKEN_TILES):
-            finish_rows(t)
+
+        Q = quantise
+        X = xi_by_token
+        Y = y_of_round
+        YI = interleave_y
+
+        def B(r):
+            spread_b(r, nc.scalar.copy)
+
+        VP(0, 0)
+        W(1, [3])
+        Q(1)
+        W(2)
+        X(1, 0)
+        VP(0, 1)
+        W(3)
+        Q(2)
+        VP(0, 2)
+        B(1)
+        Q(3)
+        W(4)
+        VP(0, 3)
+        X(1, 1)
+        Y(0)
+        YI(0)
+        W(5)
+        VP(1, 0)
+        Q(4)
+        Y(1)
+        YI(1)
+        W(6)
+        VP(1, 1)
+        VP(1, 2)
+        X(2, 0)
+        Q(5)
+        B(2)
+        Y(2)
+        YI(2)
+        VP(1, 3)
+        X(2, 1)
+        W(7)
+        Q(6)
+        Y(3)
+        YI(3)
+        VP(2, 0)
+        X(3, 0)
+        B(3)
+        VP(2, 1)
+        Q(7)
+        Q(8)
+        X(3, 1)
+        spread_norm_w()
+        second_matmul()
+        VP(2, 2)
+        VP(2, 3)
+        sumsq = sums_of_squares()
+        one_over_rms(sumsq)
+        VP(3, 0)
+        VP(3, 1)
+        VP(3, 2)
+        finish_rows(0)
+        VP(3, 3)
+        finish_rows(1)

@@ -97,52 +97,86 @@ def tile_mamba3core_kernel(
         grouped_of = {}
         xi_of = {}
         y_lin_of = {}
+        product_of = {}
         acc_of = {}
         tiles_of_round = [(t, part) for t in range(TOKEN_TILES) for part in range(2)]
 
-        def load_weights(n, parts=1):
-            w_sb = staging.tile([P, 4 * CHUNK_WORDS], BF16, tag="stage")
+        def load_weights(n, halves=1):
+            if n not in loaded:
+                w_sb = staging.tile([P, 4 * CHUNK_WORDS], BF16, tag="stage")
+                loaded[n] = w_sb
             if n < ROUNDS:
-                by_row = w_sb[:].rearrange("p (j k) -> p j k", j=4)
+                by_row = loaded[n][:].rearrange("p (j k) -> p j k", j=4)
                 rows = W_in[n * CHUNK : (n + 1) * CHUNK, :].rearrange("(p j) k -> p j k", j=4)
             else:
                 first = (n - ROUNDS) * OUT_COLS
-                by_row = w_sb[:].rearrange("p (i f) -> p i f", i=2)
+                by_row = loaded[n][:].rearrange("p (i f) -> p i f", i=2)
                 rows = W_out[first : first + OUT_COLS, :].rearrange("(i p) f -> p i f", p=P)
-            width = rows.shape[2] // parts
-            for part in range(parts):
-                cols = slice(part * width, (part + 1) * width)
-                nc.sync.dma_start(out=by_row[:, :, cols], in_=rows[:, :, cols])
-            loaded[n] = w_sb
+            return by_row, rows
 
-        def k_to_partitions(rows_sb, row_tiles, passes, k_pass, grouped, copies):
-            words = rows_sb.bitcast(F32)
-            row_words = passes * PASS_WORDS
-            pairs = row_tiles // 2
-            for pair in range(pairs):
-                bank = work_banks.tile([P, BANK], F32, tag="bank")
+        def start_load(n, tiles):
+            by_row, rows = load_weights(n)
+            nc.sync.dma_start(out=by_row[:, tiles, :], in_=rows[:, tiles, :])
+
+        def load_x(t):
+            nc.sync.dma_start(
+                out=x_sb[:, t * D_MODEL : (t + 1) * D_MODEL], in_=x_rows[t * P : (t + 1) * P, :]
+            )
+
+        def x_to_partitions(t, copy):
+            words = x_sb[:].bitcast(F32)
+            bank = work_banks.tile([P, BANK], F32, tag="bank")
+            for k_pass in range(IN_PASSES):
                 for h in range(2):
-                    for s in range(2):
-                        first = (2 * pair + s) * row_words + k_pass * PASS_WORDS
-                        nc.tensor.transpose(
-                            out=bank[:, (2 * h + s) * P : (2 * h + s + 1) * P],
-                            in_=words[:, first + h : first + PASS_WORDS : 2],
-                            identity=ident[:],
-                        )
-                b = k_pass * pairs + pair
-                column = b * 2 * P
-                copies[b % len(copies)](
-                    out=grouped[:, column : column + 2 * P, :],
-                    in_=bank[:].rearrange("p (h c) -> p c h", h=2),
+                    first = t * D_MODEL // 2 + k_pass * PASS_WORDS
+                    nc.tensor.transpose(
+                        out=bank[:, (2 * k_pass + h) * P : (2 * k_pass + h + 1) * P],
+                        in_=words[:, first + h : first + PASS_WORDS : 2],
+                        identity=ident[:],
+                    )
+            copy(
+                out=x_grouped[:].rearrange("p (k c) h -> p k c h", k=IN_PASSES)[
+                    :, :, t * P : (t + 1) * P, :
+                ],
+                in_=bank[:].rearrange("p (k h c) -> p k c h", k=IN_PASSES, h=2),
+            )
+
+        def quantise_x(t):
+            for k_pass in range(IN_PASSES):
+                cols = slice(k_pass * TOKENS + t * P, k_pass * TOKENS + (t + 1) * P)
+                nc.vector.quantize_mx(
+                    out=x_codes[:, cols].bitcast(FP8X4),
+                    scales=x_scales[:, cols],
+                    in_=x_grouped[:, cols, :].rearrange("p c h -> p (c h)").bitcast(BF16),
                 )
 
-        def prepare_weights(n, copies, k_passes):
+        def bank_of_weights(n, k_pass, pair, copy):
             if n not in grouped_of:
                 grouped = grouping.tile([P, CHUNK_WORDS, 2], F32, tag="grouped", align_bytes=64)
                 grouped_of[n] = grouped
+            words = loaded[n][:].bitcast(F32)
             passes = IN_PASSES if n < ROUNDS else OUT_PASSES
-            for k_pass in k_passes:
-                k_to_partitions(loaded[n][:], 8 // passes, passes, k_pass, grouped_of[n], copies)
+            pairs = 4 // passes
+            bank = work_banks.tile([P, BANK], F32, tag="bank")
+            for h in range(2):
+                for s in range(2):
+                    first = ((2 * pair + s) * passes + k_pass) * PASS_WORDS
+                    nc.tensor.transpose(
+                        out=bank[:, (2 * h + s) * P : (2 * h + s + 1) * P],
+                        in_=words[:, first + h : first + PASS_WORDS : 2],
+                        identity=ident[:],
+                    )
+            column = (k_pass * pairs + pair) * 2 * P
+            copy(
+                out=grouped_of[n][:, column : column + 2 * P, :],
+                in_=bank[:].rearrange("p (h c) -> p c h", h=2),
+            )
+
+        def prepare_weights(n, copies):
+            passes = IN_PASSES if n < ROUNDS else OUT_PASSES
+            for b in range(4):
+                k_pass, pair = divmod(b, 4 // passes)
+                bank_of_weights(n, k_pass, pair, copies[b])
 
         def quantise(n):
             if n < ROUNDS:
@@ -157,13 +191,15 @@ def tile_mamba3core_kernel(
                 values = grouped_of[n][:].rearrange("p c h -> p (c h)").bitcast(BF16)
             nc.vector.quantize_mx(out=codes.bitcast(FP8X4), scales=scales, in_=values)
 
-        def quantise_pass_of_chunk_0(k_pass):
-            cols = slice(k_pass * CHUNK, (k_pass + 1) * CHUNK)
-            nc.vector.quantize_mx(
-                out=win_codes[:, 0, cols].bitcast(FP8X4),
-                scales=win_scales[:, 0, cols],
-                in_=grouped_of[0][:, cols, :].rearrange("p c h -> p (c h)").bitcast(BF16),
-            )
+        def quantise_half_of_chunk_0(pair):
+            for k_pass in range(IN_PASSES):
+                first = k_pass * CHUNK + pair * 2 * P
+                cols = slice(first, first + 2 * P)
+                nc.vector.quantize_mx(
+                    out=win_codes[:, 0, cols].bitcast(FP8X4),
+                    scales=win_scales[:, 0, cols],
+                    in_=grouped_of[0][:, cols, :].rearrange("p c h -> p (c h)").bitcast(BF16),
+                )
 
         def mx_pass(acc, a_codes, a_scales, b_codes, b_scales, first, last):
             nc.tensor.matmul_mx(
@@ -187,8 +223,8 @@ def tile_mamba3core_kernel(
                 )
             copy(out=dest, in_=bank[:])
 
-        def spread_b(r, copy):
-            for part in range(2):
+        def spread_b(r, copy, parts=range(2)):
+            for part in parts:
                 for h in range(2):
                     block = 2 * r + h
                     spread_rows(
@@ -198,51 +234,56 @@ def tile_mamba3core_kernel(
                         copy,
                     )
 
-        def xi_by_token(r, t):
-            xi = xi_banks.tile([P, CHUNK], F32, tag="xi")
+        def xi_by_token(r, t, js=slice(0, 4)):
+            xi = xi_banks.tile([P, BANK], F32, tag="xi")
+            width = (js.stop - js.start) * P
             for k_pass in range(IN_PASSES):
                 toks = slice(k_pass * TOKENS + t * P, k_pass * TOKENS + (t + 1) * P)
-                feats = slice(k_pass * CHUNK, (k_pass + 1) * CHUNK)
+                first = k_pass * CHUNK + js.start * P
                 mx_pass(
-                    xi[:],
+                    xi[:, 0:width],
                     x_codes[:, toks],
                     x_scales[:, toks],
-                    win_codes[:, r, feats],
-                    win_scales[:, r, feats],
+                    win_codes[:, r, first : first + width],
+                    win_scales[:, r, first : first + width],
                     k_pass == 0,
                     k_pass == IN_PASSES - 1,
                 )
-            xi_of[(r, t)] = xi
-
-        def b_values(r, h, part):
-            width = 2 * P * STATES
-            first = (2 * r + h) * width
-            return b_all[part][:].bitcast(BF16)[:, first : first + width]
-
-        def store_products(r, t, part, prod):
-            nc.sync.dma_start(
-                out=state_rows[part][
-                    t * P : (t + 1) * P, r * CHUNK * STATES : (r + 1) * CHUNK * STATES
-                ],
-                in_=prod[:],
+            xi_of.setdefault((r, t), []).append(
+                (js, xi[:, 0:width].rearrange("t (j q) -> t q j", q=P))
             )
 
-        def state_products(r, t, part):
-            prod = staging.tile([P, CHUNK * STATES], F32, tag="stage")
-            width = 2 * P * STATES
-            for h in range(2):
-                xi_quads = xi_of[(r, t)][:].rearrange("t (j q) -> t q j", j=4)[
-                    :, h * P // 2 : (h + 1) * P // 2, :
-                ]
-                nc.vector.tensor_tensor(
-                    out=prod[:, h * width : (h + 1) * width].rearrange(
-                        "t (q j n) -> t q j n", j=4, n=STATES
-                    ),
-                    in0=xi_quads.unsqueeze(3).to_broadcast([P, P // 2, 4, STATES]),
-                    in1=b_values(r, h, part).rearrange("t (q j n) -> t q j n", j=4, n=STATES),
-                    op=ALU.mult,
-                )
-            store_products(r, t, part, prod)
+        def store_products(r, t, part, qs=slice(0, P)):
+            width = 4 * STATES
+            first = r * CHUNK * STATES
+            nc.sync.dma_start(
+                out=state_rows[part][
+                    t * P : (t + 1) * P, first + qs.start * width : first + qs.stop * width
+                ],
+                in_=product_of[(r, t, part)][:, qs.start * width : qs.stop * width],
+            )
+
+        def products(r, t, part, piece, qs):
+            if (r, t, part) not in product_of:
+                prod = staging.tile([P, CHUNK * STATES], F32, tag="stage")
+                product_of[(r, t, part)] = prod
+            js, xi = xi_of[(r, t)][piece]
+            shape = [P, qs.stop - qs.start, js.stop - js.start, STATES]
+            first = r * CHUNK * STATES
+            b_values = b_all[part][:].bitcast(BF16)[:, first : first + CHUNK * STATES]
+            nc.vector.tensor_tensor(
+                out=product_of[(r, t, part)][:].rearrange("t (q j n) -> t q j n", j=4, n=STATES)[
+                    :, qs, js, :
+                ],
+                in0=xi[:, qs, :].unsqueeze(3).to_broadcast(shape),
+                in1=b_values.rearrange("t (q j n) -> t q j n", j=4, n=STATES)[:, qs, js, :],
+                op=ALU.mult,
+            )
+
+        def product_tile(r, t, part, cuts=2):
+            width = P // cuts
+            for c in range(cuts):
+                products(r, t, part, 0, slice(c * width, (c + 1) * width))
 
         def gain_on_partitions():
             for part in range(2):
@@ -294,15 +335,11 @@ def tile_mamba3core_kernel(
             y_lin_of[r] = y_lin
 
         def interleave_y(r):
-            nc.gpsimd.tensor_scalar(
+            nc.scalar.copy(
                 out=y_grouped[:, r * 4 * TOKENS : (r + 1) * 4 * TOKENS].rearrange(
                     "p (t j) -> p t j", j=4
                 ),
-                in0=y_lin_of[r][:].rearrange("p j t -> p t j"),
-                scalar1=1.0,
-                scalar2=0.0,
-                op0=ALU.mult,
-                op1=ALU.add,
+                in_=y_lin_of[r][:].rearrange("p j t -> p t j"),
             )
 
         def second_matmul():
@@ -396,55 +433,67 @@ def tile_mamba3core_kernel(
                 out=table[part * TABLE_ROWS : (part + 1) * TABLE_ROWS, :],
                 in_=b_flat[part].rearrange("(r w) -> r w", w=TABLE_ROW),
             )
-        nc.sync.dma_start(
-            out=x_sb[:].rearrange("p (t k) -> p t k", t=TOKEN_TILES),
-            in_=x_rows.rearrange("(t p) k -> p t k", p=P),
-        )
-        load_weights(0, parts=IN_PASSES)
-        load_weights(1)
-        for part in range(2):
-            nc.sync.dma_start(
-                out=b_feats[:, part, :, :],
-                in_=b_flat[part].rearrange("(r p w) -> p r w", p=P, w=4 * STATES),
-            )
-            nc.sync.dma_start(
-                out=c_feats[:, part, :, :],
-                in_=c_flat[part].rearrange("(r p w) -> p r w", p=P, w=4 * STATES),
-            )
-        for n in range(2, WEIGHT_CHUNKS):
-            load_weights(n)
+        load_x(0)
+        start_load(0, slice(0, 2))
+        load_x(1)
+        start_load(0, slice(2, 4))
+        for n in range(1, WEIGHT_CHUNKS):
+            start_load(n, slice(0, 4) if n < ROUNDS else slice(0, 2))
+            if n == ROUNDS:
+                for part in range(2):
+                    nc.sync.dma_start(
+                        out=b_feats[:, part, :, :],
+                        in_=b_flat[part].rearrange("(r p w) -> p r w", p=P, w=4 * STATES),
+                    )
+                    nc.sync.dma_start(
+                        out=c_feats[:, part, :, :],
+                        in_=c_flat[part].rearrange("(r p w) -> p r w", p=P, w=4 * STATES),
+                    )
         nc.sync.dma_start(
             out=norm_w_rows[0:NORM_W_ROWS, :], in_=norm_w.rearrange("(r w) -> r w", w=TABLE_ROW)
         )
 
         gain_on_partitions()
 
-        both = [nc.scalar.copy, nc.vector.tensor_copy]
-        for k_pass in range(IN_PASSES):
-            k_to_partitions(x_sb[:], TOKEN_TILES, IN_PASSES, k_pass, x_grouped, both)
-        prepare_weights(0, both, [0])
-        nc.vector.quantize_mx(
-            out=x_codes[:].bitcast(FP8X4),
-            scales=x_scales[:],
-            in_=x_grouped[:].rearrange("p c h -> p (c h)").bitcast(BF16),
-        )
-        quantise_pass_of_chunk_0(0)
+        x_to_partitions(0, nc.vector.tensor_copy)
         bank = work_banks.tile([P, BANK], F32, tag="bank")
         nc.tensor.transpose(out=bank[:, 0:P], in_=table[:].bitcast(F32), identity=ident[:])
         nc.scalar.copy(out=table_columns[:], in_=bank[:, 0:P])
-        prepare_weights(0, both, [1])
-        quantise_pass_of_chunk_0(1)
-        spread_b(0, nc.scalar.copy)
-        xi_by_token(0, 0)
+        bank_of_weights(0, 0, 0, nc.scalar.copy)
+        bank_of_weights(0, 1, 0, nc.vector.tensor_copy)
+        quantise_x(0)
+        quantise_half_of_chunk_0(0)
+        spread_b(0, nc.scalar.copy, [0])
+        x_to_partitions(1, nc.vector.tensor_copy)
+        xi_by_token(0, 0, slice(0, 2))
+        products(0, 0, 0, 0, slice(0, P))
+        bank_of_weights(0, 0, 1, nc.scalar.copy)
+        bank_of_weights(0, 1, 1, nc.scalar.copy)
+        spread_b(0, nc.scalar.copy, [1])
+        quantise_x(1)
+        quantise_half_of_chunk_0(1)
+        xi_by_token(0, 0, slice(2, 4))
         xi_by_token(0, 1)
+        products(0, 0, 0, 1, slice(0, P))
+        store_products(0, 0, 0)
+        products(0, 0, 1, 0, slice(0, P))
+        products(0, 0, 1, 1, slice(0, P))
+        store_products(0, 0, 1)
 
         def W(n, v=()):
             copies = [nc.vector.tensor_copy if b in v else nc.scalar.copy for b in range(4)]
-            prepare_weights(n, copies, range(IN_PASSES if n < ROUNDS else OUT_PASSES))
+            prepare_weights(n, copies)
 
-        def VP(r, i):
+        def VP(r, i, cuts=1, stores=1):
             t, part = tiles_of_round[i]
-            state_products(r, t, part)
+            width = P // cuts
+            for c in range(cuts):
+                qs = slice(c * width, (c + 1) * width)
+                products(r, t, part, 0, qs)
+                if stores == cuts:
+                    store_products(r, t, part, qs)
+            if stores != cuts:
+                store_products(r, t, part)
 
         Q = quantise
         X = xi_by_token
@@ -454,57 +503,55 @@ def tile_mamba3core_kernel(
         def B(r):
             spread_b(r, nc.scalar.copy)
 
-        VP(0, 0)
-        W(1, [3])
-        Q(1)
+        W(1)
         W(2)
+        Q(1)
+        VP(0, 2)
         X(1, 0)
-        VP(0, 1)
         W(3)
         Q(2)
-        VP(0, 2)
         B(1)
-        Q(3)
-        W(4)
         VP(0, 3)
         X(1, 1)
+        Q(3)
+        W(4)
+        VP(1, 0)
+        X(2, 0)
+        Q(4)
         Y(0)
         YI(0)
         W(5)
-        VP(1, 0)
-        Q(4)
+        VP(1, 1)
         Y(1)
         YI(1)
-        W(6)
-        VP(1, 1)
         VP(1, 2)
-        X(2, 0)
         Q(5)
+        W(6)
         B(2)
-        Y(2)
-        YI(2)
         VP(1, 3)
         X(2, 1)
-        W(7)
+        Y(2)
+        YI(2)
         Q(6)
+        W(7)
         Y(3)
         YI(3)
         VP(2, 0)
         X(3, 0)
-        B(3)
         VP(2, 1)
+        B(3)
+        VP(2, 2)
         Q(7)
         Q(8)
         X(3, 1)
         spread_norm_w()
         second_matmul()
-        VP(2, 2)
         VP(2, 3)
+        VP(3, 0)
         sumsq = sums_of_squares()
         one_over_rms(sumsq)
-        VP(3, 0)
         VP(3, 1)
         VP(3, 2)
         finish_rows(0)
-        VP(3, 3)
         finish_rows(1)
+        VP(3, 3, 4, 4)

@@ -59,6 +59,7 @@ def tile_mamba3core_kernel(
         grouping = ctx.enter_context(tc.tile_pool(name="grouping", bufs=3))
         staging = ctx.enter_context(tc.tile_pool(name="staging", bufs=12))
         y_rows = ctx.enter_context(tc.tile_pool(name="y_rows", bufs=2))
+        xi_copies = ctx.enter_context(tc.tile_pool(name="xi_copies", bufs=2))
         small = ctx.enter_context(tc.tile_pool(name="small", bufs=2))
         xi_banks = ctx.enter_context(tc.psum_pool(name="xi_banks", bufs=3))
         work_banks = ctx.enter_context(tc.psum_pool(name="work_banks", bufs=5))
@@ -97,6 +98,7 @@ def tile_mamba3core_kernel(
         grouped_of = {}
         xi_of = {}
         y_lin_of = {}
+        gpsimd_xi = {}
         product_of = {}
         acc_of = {}
         tiles_of_round = [(t, part) for t in range(TOKEN_TILES) for part in range(2)]
@@ -280,10 +282,35 @@ def tile_mamba3core_kernel(
                 op=ALU.mult,
             )
 
-        def product_tile(r, t, part, cuts=2):
-            width = P // cuts
-            for c in range(cuts):
-                products(r, t, part, 0, slice(c * width, (c + 1) * width))
+        def xi_for_gpsimd(r):
+            xi_sb = xi_copies.tile([P, CHUNK], F32, tag="xi_sb")
+            nc.scalar.copy(
+                out=xi_sb[:].rearrange("t (q j) -> t q j", j=4),
+                in_=xi_of[(r, TOKEN_TILES - 1)][0][1],
+            )
+            gpsimd_xi[r] = xi_sb
+
+        def gpsimd_products(r, part, qs):
+            t = TOKEN_TILES - 1
+            if (r, t, part) not in product_of:
+                prod = staging.tile([P, CHUNK * STATES], F32, tag="stage")
+                product_of[(r, t, part)] = prod
+            width = 4 * STATES
+            feats = slice(qs.start * 4, qs.stop * 4)
+            first = r * CHUNK * STATES
+            b_values = b_all[part][:].bitcast(BF16)[
+                :, first + qs.start * width : first + qs.stop * width
+            ]
+            nc.gpsimd.tensor_tensor(
+                out=product_of[(r, t, part)][:, qs.start * width : qs.stop * width].rearrange(
+                    "t (f n) -> t f n", n=STATES
+                ),
+                in0=gpsimd_xi[r][:, feats]
+                .unsqueeze(2)
+                .to_broadcast([P, feats.stop - feats.start, STATES]),
+                in1=b_values.rearrange("t (f n) -> t f n", n=STATES),
+                op=ALU.mult,
+            )
 
         def gain_on_partitions():
             for part in range(2):
@@ -335,11 +362,15 @@ def tile_mamba3core_kernel(
             y_lin_of[r] = y_lin
 
         def interleave_y(r):
-            nc.scalar.copy(
+            nc.gpsimd.tensor_scalar(
                 out=y_grouped[:, r * 4 * TOKENS : (r + 1) * 4 * TOKENS].rearrange(
                     "p (t j) -> p t j", j=4
                 ),
-                in_=y_lin_of[r][:].rearrange("p j t -> p t j"),
+                in0=y_lin_of[r][:].rearrange("p j t -> p t j"),
+                scalar1=1.0,
+                scalar2=0.0,
+                op0=ALU.mult,
+                op1=ALU.add,
             )
 
         def second_matmul():
@@ -495,6 +526,18 @@ def tile_mamba3core_kernel(
             if stores != cuts:
                 store_products(r, t, part)
 
+        def G(r, part, c, cuts=2):
+            gpsimd_products(r, part, slice(c * P // cuts, (c + 1) * P // cuts))
+
+        def VH(r, i, c, cuts=2):
+            t, part = tiles_of_round[i]
+            products(r, t, part, 0, slice(c * P // cuts, (c + 1) * P // cuts))
+
+        def ST(r, i):
+            t, part = tiles_of_round[i]
+            store_products(r, t, part)
+
+        XG = xi_for_gpsimd
         Q = quantise
         X = xi_by_token
         Y = y_of_round
@@ -514,17 +557,17 @@ def tile_mamba3core_kernel(
         VP(0, 3)
         X(1, 1)
         Q(3)
-        W(4)
         VP(1, 0)
+        W(4, [3])
         X(2, 0)
         Q(4)
+        VP(1, 1)
         Y(0)
         YI(0)
         W(5)
-        VP(1, 1)
+        VP(1, 2)
         Y(1)
         YI(1)
-        VP(1, 2)
         Q(5)
         W(6)
         B(2)
@@ -542,16 +585,16 @@ def tile_mamba3core_kernel(
         B(3)
         VP(2, 2)
         Q(7)
-        Q(8)
+        VP(2, 3)
         X(3, 1)
+        Q(8)
         spread_norm_w()
         second_matmul()
-        VP(2, 3)
         VP(3, 0)
         sumsq = sums_of_squares()
         one_over_rms(sumsq)
         VP(3, 1)
         VP(3, 2)
         finish_rows(0)
+        VP(3, 3)
         finish_rows(1)
-        VP(3, 3, 4, 4)

@@ -470,7 +470,7 @@ def tile_mamba3core_kernel(
         start_load(0, slice(2, 4))
         for n in range(1, WEIGHT_CHUNKS):
             start_load(n, slice(0, 4) if n < ROUNDS else slice(0, 2))
-            if n == ROUNDS:
+            if n == 1:
                 for part in range(2):
                     nc.sync.dma_start(
                         out=b_feats[:, part, :, :],

@@ -79,6 +79,7 @@ def tile_mamba3core_kernel(
         gain_diff = keep.tile([P, ROUNDS * 4, STATES], F32)
         gain_half = keep.tile([P, ROUNDS * 4, 2], F32)
         gain = keep.tile([P, FEATURES // P], F32)
+        sumsq = keep.tile([P, TOKEN_TILES * 2], F32)
         minus_half = keep.tile([P, TOKEN_TILES], F32)
         rstd = keep.tile([P, TOKEN_TILES], F32)
         norm_w_all = keep.tile([P, D_MODEL // 2], F32)
@@ -373,40 +374,37 @@ def tile_mamba3core_kernel(
                 op1=ALU.add,
             )
 
-        def second_matmul():
+        def second_matmul(half):
             for t in range(TOKEN_TILES):
-                for half in range(2):
-                    acc = work_banks.tile([P, BANK], F32, tag="bank")
-                    for s in range(2):
-                        chunk = 2 * half + s
-                        for k_pass in range(OUT_PASSES):
-                            toks = slice(k_pass * TOKENS + t * P, k_pass * TOKENS + (t + 1) * P)
-                            cols = slice(k_pass * OUT_COLS, (k_pass + 1) * OUT_COLS)
-                            mx_pass(
-                                acc[:, s * OUT_COLS : (s + 1) * OUT_COLS],
-                                y_codes[:, toks],
-                                y_scales[:, toks],
-                                wout_codes[:, chunk, cols],
-                                wout_scales[:, chunk, cols],
-                                k_pass == 0,
-                                k_pass == OUT_PASSES - 1,
-                            )
-                    acc_of[(t, half)] = acc
+                acc = work_banks.tile([P, BANK], F32, tag="bank")
+                acc_of[(t, half)] = acc
+            for s in range(2):
+                chunk = 2 * half + s
+                for t in range(TOKEN_TILES):
+                    for k_pass in range(OUT_PASSES):
+                        toks = slice(k_pass * TOKENS + t * P, k_pass * TOKENS + (t + 1) * P)
+                        cols = slice(k_pass * OUT_COLS, (k_pass + 1) * OUT_COLS)
+                        mx_pass(
+                            acc_of[(t, half)][:, s * OUT_COLS : (s + 1) * OUT_COLS],
+                            y_codes[:, toks],
+                            y_scales[:, toks],
+                            wout_codes[:, chunk, cols],
+                            wout_scales[:, chunk, cols],
+                            k_pass == 0,
+                            k_pass == OUT_PASSES - 1,
+                        )
 
-        def sums_of_squares():
-            sumsq = keep.tile([P, TOKEN_TILES * 2], F32)
+        def sums_of_squares(half):
             for t in range(TOKEN_TILES):
-                for half in range(2):
-                    b = 2 * t + half
-                    nc.scalar.activation(
-                        out=y_grouped[:, b * BANK : (b + 1) * BANK],
-                        in_=acc_of[(t, half)][:],
-                        func=ACT.Square,
-                        accum_out=sumsq[:, b : b + 1],
-                    )
-            return sumsq
+                b = 2 * t + half
+                nc.scalar.activation(
+                    out=y_grouped[:, b * BANK : (b + 1) * BANK],
+                    in_=acc_of[(t, half)][:],
+                    func=ACT.Square,
+                    accum_out=sumsq[:, b : b + 1],
+                )
 
-        def one_over_rms(sumsq):
+        def one_over_rms():
             total = small.tile([P, TOKEN_TILES], F32, tag="total")
             mean_eps = small.tile([P, TOKEN_TILES], F32, tag="mean_eps")
             by_half = sumsq[:].rearrange("p (t h) -> p t h", h=2)
@@ -436,15 +434,16 @@ def tile_mamba3core_kernel(
                     op0=ALU.mult,
                     op1=ALU.mult,
                 )
-            nc.vector.tensor_tensor(
-                out=final[:, D_MODEL : 2 * D_MODEL],
-                in0=final[:, 0:D_MODEL],
-                in1=x_sb[:, t * D_MODEL : (t + 1) * D_MODEL],
-                op=ALU.add,
-            )
-            nc.scalar.dma_start(
-                out=res_rows[t * P : (t + 1) * P, :], in_=final[:, D_MODEL : 2 * D_MODEL]
-            )
+            for half in range(2):
+                cols = slice(half * BANK, (half + 1) * BANK)
+                res = slice(D_MODEL + half * BANK, D_MODEL + (half + 1) * BANK)
+                nc.vector.tensor_tensor(
+                    out=final[:, res],
+                    in0=final[:, cols],
+                    in1=x_sb[:, t * D_MODEL + half * BANK : t * D_MODEL + (half + 1) * BANK],
+                    op=ALU.add,
+                )
+                nc.scalar.dma_start(out=res_rows[t * P : (t + 1) * P, cols], in_=final[:, res])
 
         def spread_norm_w():
             bank = work_banks.tile([P, BANK], F32, tag="bank")
@@ -538,6 +537,8 @@ def tile_mamba3core_kernel(
             store_products(r, t, part)
 
         XG = xi_for_gpsimd
+        M = second_matmul
+        SQ = sums_of_squares
         Q = quantise
         X = xi_by_token
         Y = y_of_round
@@ -576,25 +577,27 @@ def tile_mamba3core_kernel(
         Y(2)
         YI(2)
         Q(6)
-        W(7)
         Y(3)
         YI(3)
+        W(7)
         VP(2, 0)
+        B(3)
         X(3, 0)
         VP(2, 1)
-        B(3)
-        VP(2, 2)
-        Q(7)
-        VP(2, 3)
         X(3, 1)
+        VP(2, 2)
         Q(8)
-        spread_norm_w()
-        second_matmul()
+        M(0)
+        Q(7)
+        M(1)
+        VP(2, 3)
+        SQ(0)
         VP(3, 0)
-        sumsq = sums_of_squares()
-        one_over_rms(sumsq)
+        SQ(1)
+        spread_norm_w()
+        one_over_rms()
         VP(3, 1)
         VP(3, 2)
-        finish_rows(0)
         VP(3, 3)
+        finish_rows(0)
         finish_rows(1)

@@ -34,6 +34,8 @@ WEIGHT_CHUNKS = 2 * ROUNDS
 Y_OPERAND = WEIGHT_CHUNKS
 AHEAD = 3
 
+GAIN_ROWS = FEATURES // P
+GAIN_ROW = P * STATES
 TABLE_ROW = 2 * P
 TABLE_ROWS = FEATURES * STATES // TABLE_ROW
 NORM_W_ROWS = D_MODEL // TABLE_ROW
@@ -73,11 +75,8 @@ def tile_mamba3core_kernel(
         b_real_all = keep.tile([P, FEATURES * STATES // 2], F32)
         b_imag_all = keep.tile([P, FEATURES * STATES // 2], F32)
         b_all = [b_real_all, b_imag_all]
-        b_feats = keep.tile([P, 2, ROUNDS, 4 * STATES], BF16)
-        c_feats = keep.tile([P, 2, ROUNDS, 4 * STATES], BF16)
-        gain_terms = keep.tile([P, 2, ROUNDS * 4 * STATES], F32)
-        gain_diff = keep.tile([P, ROUNDS * 4, STATES], F32)
-        gain_half = keep.tile([P, ROUNDS * 4, 2], F32)
+        gain_rows = keep.tile([P, 4 * P], F32)
+        gates = keep.tile([P, WEIGHT_CHUNKS + 1], U32)
         gain = keep.tile([P, FEATURES // P], F32)
         sumsq = keep.tile([P, TOKEN_TILES * 2], F32)
         minus_half = keep.tile([P, TOKEN_TILES], F32)
@@ -291,6 +290,12 @@ def tile_mamba3core_kernel(
             )
             gpsimd_xi[r] = xi_sb
 
+        def gate(n):
+            codes = win_codes[:, n, :] if n < ROUNDS else wout_codes[:, n - ROUNDS, :]
+            nc.gpsimd.tensor_copy(
+                out=gates[:, n : n + 1], in_=codes[:, CHUNK_WORDS - 1 : CHUNK_WORDS]
+            )
+
         def gpsimd_products(r, part, qs):
             t = TOKEN_TILES - 1
             if (r, t, part) not in product_of:
@@ -313,26 +318,49 @@ def tile_mamba3core_kernel(
                 op=ALU.mult,
             )
 
-        def gain_on_partitions():
-            for part in range(2):
-                nc.gpsimd.tensor_tensor(
-                    out=gain_terms[:, part, :],
-                    in0=c_feats[:, part, :, :].rearrange("p r w -> p (r w)"),
-                    in1=b_feats[:, part, :, :].rearrange("p r w -> p (r w)"),
-                    op=ALU.mult,
-                )
+        def gain_in_rows():
+            b_rows = bc_rows[0:GAIN_ROWS, 0 : 2 * GAIN_ROW]
+            c_rows = bc_rows[0:GAIN_ROWS, 2 * GAIN_ROW : 4 * GAIN_ROW]
+            terms = gain_work[0:GAIN_ROWS, 0 : 2 * GAIN_ROW]
+            diff = gain_work[0:GAIN_ROWS, 2 * GAIN_ROW : 3 * GAIN_ROW]
+            half = gain_work[0:GAIN_ROWS, 3 * GAIN_ROW : 3 * GAIN_ROW + GAIN_ROW // 2].rearrange(
+                "r (f n) -> r f n", n=2
+            )
+            nc.gpsimd.tensor_tensor(out=terms, in0=c_rows, in1=b_rows, op=ALU.mult)
             nc.gpsimd.tensor_tensor(
-                out=gain_diff[:].rearrange("p f n -> p (f n)"),
-                in0=gain_terms[:, 0, :],
-                in1=gain_terms[:, 1, :],
+                out=diff,
+                in0=terms[:, 0:GAIN_ROW],
+                in1=terms[:, GAIN_ROW : 2 * GAIN_ROW],
                 op=ALU.subtract,
             )
+            by_state = diff.rearrange("r (f n) -> r f n", n=STATES)
             nc.gpsimd.tensor_tensor(
-                out=gain_half[:], in0=gain_diff[:, :, 0:2], in1=gain_diff[:, :, 2:4], op=ALU.add
+                out=half, in0=by_state[:, :, 0:2], in1=by_state[:, :, 2:4], op=ALU.add
             )
-            nc.gpsimd.tensor_tensor(
-                out=gain[:], in0=gain_half[:, :, 0], in1=gain_half[:, :, 1], op=ALU.add
-            )
+            for d in range(4):
+                nc.gpsimd.tensor_tensor(
+                    out=gain_rows[0:GAIN_ROWS, :].rearrange(
+                        "r (j d q) -> r d q j", j=4, d=4
+                    )[:, d, :, :],
+                    in0=half[:, :, 0].rearrange("r (q j) -> r q j", j=4),
+                    in1=half[:, :, 1].rearrange("r (q j) -> r q j", j=4),
+                    op=ALU.add,
+                )
+
+        def gain_to_partitions():
+            bank = work_banks.tile([P, BANK], F32, tag="bank")
+            for j in range(4):
+                nc.tensor.transpose(
+                    out=bank[:, j * P : (j + 1) * P],
+                    in_=gain_rows[:, j * P : (j + 1) * P],
+                    identity=ident[:],
+                )
+            for d in range(4):
+                own = slice(32 * d, 32 * (d + 1))
+                nc.vector.tensor_copy(
+                    out=gain[own, :].rearrange("p (r j) -> p r j", j=4),
+                    in_=bank[own, :].rearrange("p (j c) -> p c j", j=4)[:, d:GAIN_ROWS:4, :],
+                )
 
         def y_of_round(r):
             y_lin = y_rows.tile([P, 4, TOKENS], BF16, tag="y_lin")
@@ -455,6 +483,9 @@ def tile_mamba3core_kernel(
 
         make_identity(nc, ident[:])
         nc.gpsimd.memset(minus_half[:], -0.5)
+        nc.gpsimd.memset(gain_rows[:], 0.0)
+        bc_rows = staging.tile([P, 4 * CHUNK_WORDS], BF16, tag="stage")
+        gain_work = staging.tile([P, CHUNK * STATES], F32, tag="stage")
         nc.vector.memset(table[2 * TABLE_ROWS : P, :], 0.0)
         nc.vector.memset(norm_w_rows[:], 0.0)
 
@@ -470,20 +501,17 @@ def tile_mamba3core_kernel(
         for n in range(1, WEIGHT_CHUNKS):
             start_load(n, slice(0, 4) if n < ROUNDS else slice(0, 2))
             if n == 1:
-                for part in range(2):
-                    nc.sync.dma_start(
-                        out=b_feats[:, part, :, :],
-                        in_=b_flat[part].rearrange("(r p w) -> p r w", p=P, w=4 * STATES),
-                    )
-                    nc.sync.dma_start(
-                        out=c_feats[:, part, :, :],
-                        in_=c_flat[part].rearrange("(r p w) -> p r w", p=P, w=4 * STATES),
-                    )
+                for i, flat in enumerate((b_flat, c_flat)):
+                    for part in range(2):
+                        first = (2 * i + part) * GAIN_ROW
+                        nc.sync.dma_start(
+                            out=bc_rows[0:GAIN_ROWS, first : first + GAIN_ROW],
+                            in_=flat[part].rearrange("(r w) -> r w", w=GAIN_ROW),
+                        )
         nc.sync.dma_start(
             out=norm_w_rows[0:NORM_W_ROWS, :], in_=norm_w.rearrange("(r w) -> r w", w=TABLE_ROW)
         )
 
-        gain_on_partitions()
 
         x_to_partitions(0, nc.vector.tensor_copy)
         bank = work_banks.tile([P, BANK], F32, tag="bank")
@@ -502,6 +530,8 @@ def tile_mamba3core_kernel(
         spread_b(0, nc.scalar.copy, [1])
         quantise_x(1)
         quantise_half_of_chunk_0(1)
+        gate(0)
+        gain_in_rows()
         xi_by_token(0, 0, slice(2, 4))
         xi_by_token(0, 1)
         products(0, 0, 0, 1, slice(0, P))
@@ -539,6 +569,7 @@ def tile_mamba3core_kernel(
         XG = xi_for_gpsimd
         M = second_matmul
         SQ = sums_of_squares
+        GP = gain_to_partitions
         Q = quantise
         X = xi_by_token
         Y = y_of_round
@@ -558,25 +589,31 @@ def tile_mamba3core_kernel(
         VP(0, 3)
         X(1, 1)
         Q(3)
+        GP()
         VP(1, 0)
         W(4, [3])
         X(2, 0)
         Q(4)
+        gate(4)
         VP(1, 1)
         Y(0)
         YI(0)
         W(5)
         VP(1, 2)
         Y(1)
-        YI(1)
         Q(5)
+        gate(5)
+        YI(1)
         W(6)
         B(2)
         VP(1, 3)
         X(2, 1)
+        XG(2)
         Y(2)
-        YI(2)
         Q(6)
+        gate(6)
+        G(2, 1, 0)
+        YI(2)
         Y(3)
         YI(3)
         W(7)
@@ -586,18 +623,23 @@ def tile_mamba3core_kernel(
         VP(2, 1)
         X(3, 1)
         VP(2, 2)
+        XG(3)
         Q(8)
         M(0)
+        VH(2, 3, 1)
+        ST(2, 3)
         Q(7)
         M(1)
-        VP(2, 3)
+        gate(7)
+        G(3, 1, 0)
+        G(3, 1, 1)
         SQ(0)
         VP(3, 0)
         SQ(1)
         spread_norm_w()
         one_over_rms()
         VP(3, 1)
+        ST(3, 3)
         VP(3, 2)
-        VP(3, 3)
         finish_rows(0)
         finish_rows(1)

from contextlib import ExitStack

import concourse.mybir as mybir
from concourse.masks import make_identity

F32 = mybir.dt.float32
BF16 = mybir.dt.bfloat16
U32 = mybir.dt.uint32
U8 = mybir.dt.uint8
FP8X4 = mybir.dt.float8_e4m3fn_x4
ALU = mybir.AluOpType
ACT = mybir.ActivationFunctionType

P = 128
TOKENS = 256
TOKEN_TILES = TOKENS // P
D_MODEL = 1024
FEATURES = 2048
STATES = 4
EPS = 2.0**-23

K_PASS = 512
PASS_WORDS = K_PASS // 2
BANK = 512

ROUNDS = 4
CHUNK = FEATURES // ROUNDS
IN_PASSES = D_MODEL // K_PASS
OUT_PASSES = FEATURES // K_PASS
OUT_COLS = D_MODEL // ROUNDS
CHUNK_WORDS = 1024

WEIGHT_CHUNKS = 2 * ROUNDS
Y_OPERAND = WEIGHT_CHUNKS
AHEAD = 3

GAIN_ROWS = FEATURES // P
GAIN_ROW = P * STATES
TABLE_ROW = 2 * P
TABLE_ROWS = FEATURES * STATES // TABLE_ROW
NORM_W_ROWS = D_MODEL // TABLE_ROW

FLOPS = 2 * TOKENS * D_MODEL * FEATURES * 2


def tile_mamba3core_kernel(
    tc, x, W_in, W_out, A_theta, B_real, B_imag, C_real, C_imag, norm_w, out_0, out_1, out_2
):
    nc = tc.nc
    x_rows = x.flatten_outer_dims()
    res_rows = out_0.flatten_outer_dims()
    state_rows = [
        out_1.rearrange("b l c d n -> (b l) (c d n)"),
        out_2.rearrange("b l c d n -> (b l) (c d n)"),
    ]
    b_flat = [B_real.rearrange("c d n -> (c d n)"), B_imag.rearrange("c d n -> (c d n)")]
    c_flat = [C_real.rearrange("c d n -> (c d n)"), C_imag.rearrange("c d n -> (c d n)")]

    with ExitStack() as ctx:
        keep = ctx.enter_context(tc.tile_pool(name="keep", bufs=1))
        grouping = ctx.enter_context(tc.tile_pool(name="grouping", bufs=3))
        staging = ctx.enter_context(tc.tile_pool(name="staging", bufs=12))
        y_rows = ctx.enter_context(tc.tile_pool(name="y_rows", bufs=2))
        xi_copies = ctx.enter_context(tc.tile_pool(name="xi_copies", bufs=2))
        small = ctx.enter_context(tc.tile_pool(name="small", bufs=2))
        xi_banks = ctx.enter_context(tc.psum_pool(name="xi_banks", bufs=3))
        work_banks = ctx.enter_context(tc.psum_pool(name="work_banks", bufs=5))
        ctx.enter_context(tc.manual_schedule())

        ident = keep.tile([P, P], F32)
        table = keep.tile([P, TABLE_ROW], BF16)
        table_columns = keep.tile([P, P], F32)
        norm_w_rows = keep.tile([P, TABLE_ROW], BF16)
        norm_w_columns = keep.tile([P, 4], F32)
        b_real_all = keep.tile([P, FEATURES * STATES // 2], F32)
        b_imag_all = keep.tile([P, FEATURES * STATES // 2], F32)
        b_all = [b_real_all, b_imag_all]
        gain_rows = keep.tile([P, 4 * P], F32)
        gates = keep.tile([P, WEIGHT_CHUNKS + 1], U32)
        gain = keep.tile([P, FEATURES // P], F32)
        sumsq = keep.tile([P, TOKEN_TILES * 2], F32)
        minus_half = keep.tile([P, TOKEN_TILES], F32)
        rstd = keep.tile([P, TOKEN_TILES], F32)
        norm_w_all = keep.tile([P, D_MODEL // 2], F32)
        x_sb = keep.tile([P, TOKEN_TILES * D_MODEL], BF16)
        x_grouped = keep.tile([P, IN_PASSES * TOKENS, 2], F32, align_bytes=64)
        y_grouped = keep.tile([P, OUT_PASSES * TOKENS * 4], BF16, align_bytes=64)
        x_codes = keep.tile([P, IN_PASSES * TOKENS], U32, align_bytes=64)
        x_scales = keep.tile([P, IN_PASSES * TOKENS], U8, align_bytes=64)
        y_codes = keep.tile([P, OUT_PASSES * TOKENS], U32, align_bytes=64)
        y_scales = keep.tile([P, OUT_PASSES * TOKENS], U8, align_bytes=64)
        win_codes = keep.tile([P, ROUNDS, CHUNK_WORDS], U32, align_bytes=64)
        win_scales = keep.tile([P, ROUNDS, CHUNK_WORDS], U8, align_bytes=64)
        wout_codes = keep.tile([P, ROUNDS, CHUNK_WORDS], U32, align_bytes=64)
        wout_scales = keep.tile([P, ROUNDS, CHUNK_WORDS], U8, align_bytes=64)

        loaded = {}
        grouped_of = {}
        xi_of = {}
        y_lin_of = {}
        gpsimd_xi = {}
        product_of = {}
        acc_of = {}
        tiles_of_round = [(t, part) for t in range(TOKEN_TILES) for part in range(2)]

        def load_weights(n, halves=1):
            if n not in loaded:
                w_sb = staging.tile([P, 4 * CHUNK_WORDS], BF16, tag="stage")
                loaded[n] = w_sb
            if n < ROUNDS:
                by_row = loaded[n][:].rearrange("p (j k) -> p j k", j=4)
                rows = W_in[n * CHUNK : (n + 1) * CHUNK, :].rearrange("(p j) k -> p j k", j=4)
            else:
                first = (n - ROUNDS) * OUT_COLS
                by_row = loaded[n][:].rearrange("p (i f) -> p i f", i=2)
                rows = W_out[first : first + OUT_COLS, :].rearrange("(i p) f -> p i f", p=P)
            return by_row, rows

        def start_load(n, tiles):
            by_row, rows = load_weights(n)
            nc.sync.dma_start(out=by_row[:, tiles, :], in_=rows[:, tiles, :])

        def load_x(t):
            nc.sync.dma_start(
                out=x_sb[:, t * D_MODEL : (t + 1) * D_MODEL], in_=x_rows[t * P : (t + 1) * P, :]
            )

        def x_to_partitions(t, copy):
            words = x_sb[:].bitcast(F32)
            bank = work_banks.tile([P, BANK], F32, tag="bank")
            for k_pass in range(IN_PASSES):
                for h in range(2):
                    first = t * D_MODEL // 2 + k_pass * PASS_WORDS
                    nc.tensor.transpose(
                        out=bank[:, (2 * k_pass + h) * P : (2 * k_pass + h + 1) * P],
                        in_=words[:, first + h : first + PASS_WORDS : 2],
                        identity=ident[:],
                    )
            copy(
                out=x_grouped[:].rearrange("p (k c) h -> p k c h", k=IN_PASSES)[
                    :, :, t * P : (t + 1) * P, :
                ],
                in_=bank[:].rearrange("p (k h c) -> p k c h", k=IN_PASSES, h=2),
            )

        def quantise_x(t):
            for k_pass in range(IN_PASSES):
                cols = slice(k_pass * TOKENS + t * P, k_pass * TOKENS + (t + 1) * P)
                nc.vector.quantize_mx(
                    out=x_codes[:, cols].bitcast(FP8X4),
                    scales=x_scales[:, cols],
                    in_=x_grouped[:, cols, :].rearrange("p c h -> p (c h)").bitcast(BF16),
                )

        def bank_of_weights(n, k_pass, pair, copy):
            if n not in grouped_of:
                grouped = grouping.tile([P, CHUNK_WORDS, 2], F32, tag="grouped", align_bytes=64)
                grouped_of[n] = grouped
            words = loaded[n][:].bitcast(F32)
            passes = IN_PASSES if n < ROUNDS else OUT_PASSES
            pairs = 4 // passes
            bank = work_banks.tile([P, BANK], F32, tag="bank")
            for h in range(2):
                for s in range(2):
                    first = ((2 * pair + s) * passes + k_pass) * PASS_WORDS
                    nc.tensor.transpose(
                        out=bank[:, (2 * h + s) * P : (2 * h + s + 1) * P],
                        in_=words[:, first + h : first + PASS_WORDS : 2],
                        identity=ident[:],
                    )
            column = (k_pass * pairs + pair) * 2 * P
            copy(
                out=grouped_of[n][:, column : column + 2 * P, :],
                in_=bank[:].rearrange("p (h c) -> p c h", h=2),
            )

        def prepare_weights(n, copies):
            passes = IN_PASSES if n < ROUNDS else OUT_PASSES
            for b in range(4):
                k_pass, pair = divmod(b, 4 // passes)
                bank_of_weights(n, k_pass, pair, copies[b])

        def quantise(n):
            if n < ROUNDS:
                codes, scales = win_codes[:, n, :], win_scales[:, n, :]
            elif n < WEIGHT_CHUNKS:
                codes, scales = wout_codes[:, n - ROUNDS, :], wout_scales[:, n - ROUNDS, :]
            else:
                codes, scales = y_codes[:], y_scales[:]
            if n == Y_OPERAND:
                values = y_grouped[:]
            else:
                values = grouped_of[n][:].rearrange("p c h -> p (c h)").bitcast(BF16)
            nc.vector.quantize_mx(out=codes.bitcast(FP8X4), scales=scales, in_=values)

        def quantise_half_of_chunk_0(pair):
            for k_pass in range(IN_PASSES):
                first = k_pass * CHUNK + pair * 2 * P
                cols = slice(first, first + 2 * P)
                nc.vector.quantize_mx(
                    out=win_codes[:, 0, cols].bitcast(FP8X4),
                    scales=win_scales[:, 0, cols],
                    in_=grouped_of[0][:, cols, :].rearrange("p c h -> p (c h)").bitcast(BF16),
                )

        def mx_pass(acc, a_codes, a_scales, b_codes, b_scales, first, last):
            nc.tensor.matmul_mx(
                out=acc,
                lhsT=a_codes.bitcast(FP8X4),
                lhsT_scale=a_scales,
                rhs=b_codes.bitcast(FP8X4),
                rhs_scale=b_scales,
                start=first,
                stop=last,
            )

        def spread_rows(columns, first_row, dest, copy):
            bank = work_banks.tile([P, BANK], F32, tag="bank")
            for i in range(4):
                row = first_row + i
                nc.tensor.transpose(
                    out=bank[:, i * P : (i + 1) * P],
                    in_=columns[:, row : row + 1].to_broadcast([P, P]),
                    identity=ident[:],
                )
            copy(out=dest, in_=bank[:])

        def spread_b(r, copy, parts=range(2)):
            for part in parts:
                for h in range(2):
                    block = 2 * r + h
                    spread_rows(
                        table_columns,
                        part * TABLE_ROWS + 4 * block,
                        b_all[part][:, block * BANK : (block + 1) * BANK],
                        copy,
                    )

        def xi_by_token(r, t, js=slice(0, 4)):
            xi = xi_banks.tile([P, BANK], F32, tag="xi")
            width = (js.stop - js.start) * P
            for k_pass in range(IN_PASSES):
                toks = slice(k_pass * TOKENS + t * P, k_pass * TOKENS + (t + 1) * P)
                first = k_pass * CHUNK + js.start * P
                mx_pass(
                    xi[:, 0:width],
                    x_codes[:, toks],
                    x_scales[:, toks],
                    win_codes[:, r, first : first + width],
                    win_scales[:, r, first : first + width],
                    k_pass == 0,
                    k_pass == IN_PASSES - 1,
                )
            xi_of.setdefault((r, t), []).append(
                (js, xi[:, 0:width].rearrange("t (j q) -> t q j", q=P))
            )

        def store_products(r, t, part, qs=slice(0, P)):
            width = 4 * STATES
            first = r * CHUNK * STATES
            nc.sync.dma_start(
                out=state_rows[part][
                    t * P : (t + 1) * P, first + qs.start * width : first + qs.stop * width
                ],
                in_=product_of[(r, t, part)][:, qs.start * width : qs.stop * width],
            )

        def products(r, t, part, piece, qs):
            if (r, t, part) not in product_of:
                prod = staging.tile([P, CHUNK * STATES], F32, tag="stage")
                product_of[(r, t, part)] = prod
            js, xi = xi_of[(r, t)][piece]
            shape = [P, qs.stop - qs.start, js.stop - js.start, STATES]
            first = r * CHUNK * STATES
            b_values = b_all[part][:].bitcast(BF16)[:, first : first + CHUNK * STATES]
            nc.vector.tensor_tensor(
                out=product_of[(r, t, part)][:].rearrange("t (q j n) -> t q j n", j=4, n=STATES)[
                    :, qs, js, :
                ],
                in0=xi[:, qs, :].unsqueeze(3).to_broadcast(shape),
                in1=b_values.rearrange("t (q j n) -> t q j n", j=4, n=STATES)[:, qs, js, :],
                op=ALU.mult,
            )

        def xi_for_gpsimd(r):
            xi_sb = xi_copies.tile([P, CHUNK], F32, tag="xi_sb")
            nc.scalar.copy(
                out=xi_sb[:].rearrange("t (q j) -> t q j", j=4),
                in_=xi_of[(r, TOKEN_TILES - 1)][0][1],
            )
            gpsimd_xi[r] = xi_sb

        def gate(n):
            codes = win_codes[:, n, :] if n < ROUNDS else wout_codes[:, n - ROUNDS, :]
            nc.gpsimd.tensor_copy(
                out=gates[:, n : n + 1], in_=codes[:, CHUNK_WORDS - 1 : CHUNK_WORDS]
            )

        def gpsimd_products(r, part, qs):
            t = TOKEN_TILES - 1
            if (r, t, part) not in product_of:
                prod = staging.tile([P, CHUNK * STATES], F32, tag="stage")
                product_of[(r, t, part)] = prod
            width = 4 * STATES
            feats = slice(qs.start * 4, qs.stop * 4)
            first = r * CHUNK * STATES
            b_values = b_all[part][:].bitcast(BF16)[
                :, first + qs.start * width : first + qs.stop * width
            ]
            nc.gpsimd.tensor_tensor(
                out=product_of[(r, t, part)][:, qs.start * width : qs.stop * width].rearrange(
                    "t (f n) -> t f n", n=STATES
                ),
                in0=gpsimd_xi[r][:, feats]
                .unsqueeze(2)
                .to_broadcast([P, feats.stop - feats.start, STATES]),
                in1=b_values.rearrange("t (f n) -> t f n", n=STATES),
                op=ALU.mult,
            )

        def gain_in_rows():
            b_rows = bc_rows[0:GAIN_ROWS, 0 : 2 * GAIN_ROW]
            c_rows = bc_rows[0:GAIN_ROWS, 2 * GAIN_ROW : 4 * GAIN_ROW]
            terms = gain_work[0:GAIN_ROWS, 0 : 2 * GAIN_ROW]
            diff = gain_work[0:GAIN_ROWS, 2 * GAIN_ROW : 3 * GAIN_ROW]
            half = gain_work[0:GAIN_ROWS, 3 * GAIN_ROW : 3 * GAIN_ROW + GAIN_ROW // 2].rearrange(
                "r (f n) -> r f n", n=2
            )
            nc.gpsimd.tensor_tensor(out=terms, in0=c_rows, in1=b_rows, op=ALU.mult)
            nc.gpsimd.tensor_tensor(
                out=diff,
                in0=terms[:, 0:GAIN_ROW],
                in1=terms[:, GAIN_ROW : 2 * GAIN_ROW],
                op=ALU.subtract,
            )
            by_state = diff.rearrange("r (f n) -> r f n", n=STATES)
            nc.gpsimd.tensor_tensor(
                out=half, in0=by_state[:, :, 0:2], in1=by_state[:, :, 2:4], op=ALU.add
            )
            for d in range(4):
                nc.gpsimd.tensor_tensor(
                    out=gain_rows[0:GAIN_ROWS, :].rearrange(
                        "r (j d q) -> r d q j", j=4, d=4
                    )[:, d, :, :],
                    in0=half[:, :, 0].rearrange("r (q j) -> r q j", j=4),
                    in1=half[:, :, 1].rearrange("r (q j) -> r q j", j=4),
                    op=ALU.add,
                )

        def gain_to_partitions():
            bank = work_banks.tile([P, BANK], F32, tag="bank")
            for j in range(4):
                nc.tensor.transpose(
                    out=bank[:, j * P : (j + 1) * P],
                    in_=gain_rows[:, j * P : (j + 1) * P],
                    identity=ident[:],
                )
            for d in range(4):
                own = slice(32 * d, 32 * (d + 1))
                nc.vector.tensor_copy(
                    out=gain[own, :].rearrange("p (r j) -> p r j", j=4),
                    in_=bank[own, :].rearrange("p (j c) -> p c j", j=4)[:, d:GAIN_ROWS:4, :],
                )

        def y_of_round(r):
            y_lin = y_rows.tile([P, 4, TOKENS], BF16, tag="y_lin")
            for pair in range(2):
                bank = work_banks.tile([P, BANK], F32, tag="bank")
                for s in range(2):
                    j = 2 * pair + s
                    for k_pass in range(IN_PASSES):
                        feats = slice(k_pass * CHUNK + j * P, k_pass * CHUNK + (j + 1) * P)
                        toks = slice(k_pass * TOKENS, (k_pass + 1) * TOKENS)
                        mx_pass(
                            bank[:, s * TOKENS : (s + 1) * TOKENS],
                            win_codes[:, r, feats],
                            win_scales[:, r, feats],
                            x_codes[:, toks],
                            x_scales[:, toks],
                            k_pass == 0,
                            k_pass == IN_PASSES - 1,
                        )
                for s in range(2):
                    j = 2 * pair + s
                    nc.scalar.activation(
                        out=y_lin[:, j, :],
                        in_=bank[:, s * TOKENS : (s + 1) * TOKENS],
                        func=ACT.Copy,
                        scale=gain[:, 4 * r + j : 4 * r + j + 1],
                    )
            y_lin_of[r] = y_lin

        def interleave_y(r):
            nc.gpsimd.tensor_scalar(
                out=y_grouped[:, r * 4 * TOKENS : (r + 1) * 4 * TOKENS].rearrange(
                    "p (t j) -> p t j", j=4
                ),
                in0=y_lin_of[r][:].rearrange("p j t -> p t j"),
                scalar1=1.0,
                scalar2=0.0,
                op0=ALU.mult,
                op1=ALU.add,
            )

        def second_matmul(half):
            for t in range(TOKEN_TILES):
                acc = work_banks.tile([P, BANK], F32, tag="bank")
                acc_of[(t, half)] = acc
            for s in range(2):
                chunk = 2 * half + s
                for t in range(TOKEN_TILES):
                    for k_pass in range(OUT_PASSES):
                        toks = slice(k_pass * TOKENS + t * P, k_pass * TOKENS + (t + 1) * P)
                        cols = slice(k_pass * OUT_COLS, (k_pass + 1) * OUT_COLS)
                        mx_pass(
                            acc_of[(t, half)][:, s * OUT_COLS : (s + 1) * OUT_COLS],
                            y_codes[:, toks],
                            y_scales[:, toks],
                            wout_codes[:, chunk, cols],
                            wout_scales[:, chunk, cols],
                            k_pass == 0,
                            k_pass == OUT_PASSES - 1,
                        )

        def sums_of_squares(half):
            for t in range(TOKEN_TILES):
                b = 2 * t + half
                nc.scalar.activation(
                    out=y_grouped[:, b * BANK : (b + 1) * BANK],
                    in_=acc_of[(t, half)][:],
                    func=ACT.Square,
                    accum_out=sumsq[:, b : b + 1],
                )

        def one_over_rms():
            total = small.tile([P, TOKEN_TILES], F32, tag="total")
            mean_eps = small.tile([P, TOKEN_TILES], F32, tag="mean_eps")
            by_half = sumsq[:].rearrange("p (t h) -> p t h", h=2)
            nc.gpsimd.tensor_tensor(
                out=total[:], in0=by_half[:, :, 0], in1=by_half[:, :, 1], op=ALU.add
            )
            nc.gpsimd.tensor_scalar(
                out=mean_eps[:],
                in0=total[:],
                scalar1=1.0 / D_MODEL,
                scalar2=EPS,
                op0=ALU.mult,
                op1=ALU.add,
            )
            nc.gpsimd.tensor_tensor(out=rstd[:], in0=mean_eps[:], in1=minus_half[:], op=ALU.pow)

        def finish_rows(t):
            final = staging.tile([P, 2 * D_MODEL], F32, tag="stage")
            norm_w_values = norm_w_all[:].bitcast(BF16)
            for half in range(2):
                cols = slice(half * BANK, (half + 1) * BANK)
                nc.vector.scalar_tensor_tensor(
                    out=final[:, cols],
                    in0=acc_of[(t, half)][:],
                    scalar=rstd[:, t : t + 1],
                    in1=norm_w_values[:, cols],
                    op0=ALU.mult,
                    op1=ALU.mult,
                )
            for half in range(2):
                cols = slice(half * BANK, (half + 1) * BANK)
                res = slice(D_MODEL + half * BANK, D_MODEL + (half + 1) * BANK)
                nc.vector.tensor_tensor(
                    out=final[:, res],
                    in0=final[:, cols],
                    in1=x_sb[:, t * D_MODEL + half * BANK : t * D_MODEL + (half + 1) * BANK],
                    op=ALU.add,
                )
                nc.scalar.dma_start(out=res_rows[t * P : (t + 1) * P, cols], in_=final[:, res])

        def spread_norm_w():
            bank = work_banks.tile([P, BANK], F32, tag="bank")
            nc.tensor.transpose(
                out=bank[:, 0:P], in_=norm_w_rows[:].bitcast(F32), identity=ident[:]
            )
            nc.scalar.copy(out=norm_w_columns[:], in_=bank[:, 0:NORM_W_ROWS])
            spread_rows(norm_w_columns, 0, norm_w_all[:], nc.scalar.copy)

        make_identity(nc, ident[:])
        nc.gpsimd.memset(minus_half[:], -0.5)
        nc.gpsimd.memset(gain_rows[:], 0.0)
        bc_rows = staging.tile([P, 4 * CHUNK_WORDS], BF16, tag="stage")
        gain_work = staging.tile([P, CHUNK * STATES], F32, tag="stage")
        nc.vector.memset(table[2 * TABLE_ROWS : P, :], 0.0)
        nc.vector.memset(norm_w_rows[:], 0.0)

        for part in range(2):
            nc.scalar.dma_start(
                out=table[part * TABLE_ROWS : (part + 1) * TABLE_ROWS, :],
                in_=b_flat[part].rearrange("(r w) -> r w", w=TABLE_ROW),
            )
        load_x(0)
        start_load(0, slice(0, 2))
        load_x(1)
        start_load(0, slice(2, 4))
        for n in range(1, WEIGHT_CHUNKS):
            start_load(n, slice(0, 4) if n < ROUNDS else slice(0, 2))
            if n == 1:
                for i, flat in enumerate((b_flat, c_flat)):
                    for part in range(2):
                        first = (2 * i + part) * GAIN_ROW
                        nc.sync.dma_start(
                            out=bc_rows[0:GAIN_ROWS, first : first + GAIN_ROW],
                            in_=flat[part].rearrange("(r w) -> r w", w=GAIN_ROW),
                        )
        nc.sync.dma_start(
            out=norm_w_rows[0:NORM_W_ROWS, :], in_=norm_w.rearrange("(r w) -> r w", w=TABLE_ROW)
        )


        x_to_partitions(0, nc.vector.tensor_copy)
        bank = work_banks.tile([P, BANK], F32, tag="bank")
        nc.tensor.transpose(out=bank[:, 0:P], in_=table[:].bitcast(F32), identity=ident[:])
        nc.scalar.copy(out=table_columns[:], in_=bank[:, 0:P])
        bank_of_weights(0, 0, 0, nc.scalar.copy)
        bank_of_weights(0, 1, 0, nc.vector.tensor_copy)
        quantise_x(0)
        quantise_half_of_chunk_0(0)
        spread_b(0, nc.scalar.copy, [0])
        x_to_partitions(1, nc.vector.tensor_copy)
        xi_by_token(0, 0, slice(0, 2))
        products(0, 0, 0, 0, slice(0, P))
        bank_of_weights(0, 0, 1, nc.scalar.copy)
        bank_of_weights(0, 1, 1, nc.scalar.copy)
        spread_b(0, nc.scalar.copy, [1])
        quantise_x(1)
        quantise_half_of_chunk_0(1)
        gate(0)
        gain_in_rows()
        xi_by_token(0, 0, slice(2, 4))
        xi_by_token(0, 1)
        products(0, 0, 0, 1, slice(0, P))
        store_products(0, 0, 0)
        products(0, 0, 1, 0, slice(0, P))
        products(0, 0, 1, 1, slice(0, P))
        store_products(0, 0, 1)

        def W(n, v=()):
            copies = [nc.vector.tensor_copy if b in v else nc.scalar.copy for b in range(4)]
            prepare_weights(n, copies)

        def VP(r, i, cuts=1, stores=1):
            t, part = tiles_of_round[i]
            width = P // cuts
            for c in range(cuts):
                qs = slice(c * width, (c + 1) * width)
                products(r, t, part, 0, qs)
                if stores == cuts:
                    store_products(r, t, part, qs)
            if stores != cuts:
                store_products(r, t, part)

        def G(r, part, c, cuts=2):
            gpsimd_products(r, part, slice(c * P // cuts, (c + 1) * P // cuts))

        def VH(r, i, c, cuts=2):
            t, part = tiles_of_round[i]
            products(r, t, part, 0, slice(c * P // cuts, (c + 1) * P // cuts))

        def ST(r, i):
            t, part = tiles_of_round[i]
            store_products(r, t, part)

        XG = xi_for_gpsimd
        M = second_matmul
        SQ = sums_of_squares
        GP = gain_to_partitions
        Q = quantise
        X = xi_by_token
        Y = y_of_round
        YI = interleave_y

        def B(r):
            spread_b(r, nc.scalar.copy)

        W(1)
        W(2)
        Q(1)
        VP(0, 2)
        X(1, 0)
        W(3)
        Q(2)
        B(1)
        VP(0, 3)
        X(1, 1)
        Q(3)
        GP()
        VP(1, 0)
        W(4, [3])
        X(2, 0)
        Q(4)
        gate(4)
        VP(1, 1)
        Y(0)
        YI(0)
        W(5)
        VP(1, 2)
        Y(1)
        Q(5)
        gate(5)
        YI(1)
        W(6)
        B(2)
        VP(1, 3)
        X(2, 1)
        XG(2)
        Y(2)
        Q(6)
        gate(6)
        G(2, 1, 0)
        YI(2)
        Y(3)
        YI(3)
        W(7)
        VP(2, 0)
        B(3)
        X(3, 0)
        VP(2, 1)
        X(3, 1)
        VP(2, 2)
        XG(3)
        Q(8)
        M(0)
        VH(2, 3, 1)
        ST(2, 3)
        Q(7)
        M(1)
        gate(7)
        G(3, 1, 0)
        G(3, 1, 1)
        SQ(0)
        VP(3, 0)
        SQ(1)
        spread_norm_w()
        one_over_rms()
        VP(3, 1)
        ST(3, 3)
        VP(3, 2)
        finish_rows(0)
        finish_rows(1)
